import numpy as np
import ml_dtypes


def mxq(x, axis, fmt="e4m3"):
    dtype, down = {"e4m3": (ml_dtypes.float8_e4m3fn, 7), "e5m2": (ml_dtypes.float8_e5m2, 14)}[fmt]
    v = np.moveaxis(np.asarray(x, np.float32).astype(ml_dtypes.bfloat16).astype(np.float64), axis, -1)
    blocks = v.reshape(v.shape[:-1] + (-1, 32))
    amax = np.abs(blocks).max(-1, keepdims=True)
    byte = np.maximum(np.where(amax > 0, np.frexp(amax)[1] - 1 + 127, 0) - down, 1)
    scale = np.exp2(byte - 127.0)
    codes = (blocks / scale).astype(np.float32).astype(dtype).astype(np.float64)
    return np.moveaxis((codes * scale).reshape(v.shape), -1, axis)


WIDE = False


def mx_kscale(k):
    if not WIDE:
        return np.ones(k)
    levels = np.array([10, -10, 5, -5, 0])
    if k % 512:
        return np.exp2(np.random.permutation(np.resize(levels, k // 32))).repeat(32)
    a = np.empty((k // 512, 16))
    for p in range(k // 512):
        a[p, :8] = np.random.permutation(np.resize(levels, 8))
        for g in range(8):
            far = levels[np.abs(levels - a[p, g]) >= 10]
            a[p, g + 8] = far[np.random.randint(len(far))]
    return np.exp2(a.ravel()).repeat(32)


BF16 = ml_dtypes.bfloat16


def bf(x):
    return np.asarray(x, np.float32).astype(BF16)


def f64(x):
    return np.asarray(x).astype(np.float64)


B, D, U, R = 3072, 512, 512, 8
EPS = 1e-12


def softplus(v):
    return np.maximum(v, 0.0) + np.log(1.0 + np.exp(-np.abs(v)))


def draw(n, p):
    v = 0.3 * np.random.standard_normal((n, D)) / np.sqrt(D)
    for r in range(R):
        v = v + 0.8 * np.random.standard_normal((n, 1)) * p[r] / np.sqrt(R * D)
    return v


def setup_inputs():
    s = mx_kscale(B)
    u = mx_kscale(U)
    p = np.random.standard_normal((R, D))
    x0 = bf(draw(B, p))
    c0 = bf(draw(U, p))
    gamma_raw = bf(np.log(np.exp(1.0) - 1.0) + 0.3 * np.random.standard_normal(U))
    g = bf(8.0 * np.random.standard_normal((B, U)) * np.exp2(np.random.randint(-6, 1, (B, 1))) / s[:, None] * u[None, :])
    xf, cf = f64(x0), f64(c0)
    x_norm = np.sum(np.square(xf), axis=-1, keepdims=True)
    c_norm = np.sum(np.square(cf), axis=-1)
    d2 = np.maximum(x_norm - 2.0 * (xf @ cf.T) + c_norm[None, :] + EPS, 0.0)
    return {"x": bf(xf * s[:, None] / u.max()), "centers": bf(cf / u[:, None] * s.min()), "gamma_raw": gamma_raw,
            "d2": np.asarray(d2, np.float32), "grad_out": g}


def reference(x, centers, gamma_raw, d2, grad_out):
    x, centers, d2 = f64(x), f64(centers), f64(d2)
    gamma = softplus(f64(gamma_raw))[None, :]
    dz = np.where(d2 > 0.0, -f64(grad_out) * gamma * np.exp(-gamma * d2), 0.0)
    px = mxq(dz, 1, "e5m2") @ mxq(centers, 0, "e4m3")
    pc = mxq(dz, 0, "e5m2").T @ mxq(x, 0, "e4m3")
    dx = -2.0 * px + 2.0 * x * np.sum(dz, axis=1)[:, None]
    dc = -2.0 * pc + 2.0 * centers * np.sum(dz, axis=0)[:, None]
    return dx, dc

@@ -1,0 +1,241 @@
+from contextlib import ExitStack
+
+import concourse.mybir as mybir
+from concourse.masks import make_identity
+
+B, D, U = 3072, 512, 512
+FLOPS = 2 * 2 * B * U * D
+
+F32 = mybir.dt.float32
+BF16 = mybir.dt.bfloat16
+U32 = mybir.dt.uint32
+U8 = mybir.dt.uint8
+E5X4 = mybir.dt.float8_e5m2_x4
+E4X4 = mybir.dt.float8_e4m3fn_x4
+ALU = mybir.AluOpType
+ACT = mybir.ActivationFunctionType
+
+P = 128
+PACK = 4
+GT = P * PACK
+G = B // GT
+
+
+def tile_rbflayer_v_kernel(tc, x, centers, gamma_raw, d2, grad_out, out_0, out_1):
+    nc = tc.nc
+    d2_v = d2.rearrange("(g p j) u -> g p j u", p=P, j=PACK)
+    go_v = grad_out.rearrange("(g p j) u -> g p j u", p=P, j=PACK)
+    x_v = x.rearrange("(g p j) i -> g p j i", p=P, j=PACK)
+    o0_v = out_0.rearrange("(g p j) i -> g p j i", p=P, j=PACK)
+    o1_v = out_1.rearrange("(q t) i -> q t i", t=PACK)
+
+    with ExitStack() as ctx:
+        const = ctx.enter_context(tc.tile_pool(name="const", bufs=1))
+        ld3 = ctx.enter_context(tc.tile_pool(name="ld3", bufs=3))
+        ld4 = ctx.enter_context(tc.tile_pool(name="ld4", bufs=4))
+        work = ctx.enter_context(tc.tile_pool(name="work", bufs=2))
+        outp = ctx.enter_context(tc.tile_pool(name="outp", bufs=3))
+        psum = ctx.enter_context(tc.psum_pool(name="psum", bufs=2))
+
+        graw = const.tile([P, PACK], BF16, name="graw")
+        nc.sync.dma_start(out=graw, in_=gamma_raw.rearrange("(q t) -> q t", t=PACK))
+        c_raw = const.tile([P, PACK, D], BF16, name="c_raw")
+
+        d2_t = []
+        go_t = []
+        x_t = []
+
+        def load_dz_inputs(g):
+            d2_g = ld3.tile([P, PACK, U], F32, name="d2_g")
+            nc.sync.dma_start(out=d2_g, in_=d2_v[g])
+            go_g = ld3.tile([P, PACK, U], BF16, name="go_g")
+            nc.sync.dma_start(out=go_g, in_=go_v[g])
+            d2_t.append(d2_g)
+            go_t.append(go_g)
+
+        def load_x(g):
+            x_g = ld4.tile([P, PACK, D], BF16, name="x_g")
+            nc.sync.dma_start(out=x_g, in_=x_v[g])
+            x_t.append(x_g)
+
+        warm = const.tile([P, 1], F32, name="warm")
+        nc.vector.memset(warm, 0.0)
+        nc.scalar.activation(out=warm, in_=warm, func=ACT.Exp)
+        ident = const.tile([P, P], F32, name="ident")
+        make_identity(nc, ident)
+
+        load_dz_inputs(0)
+        nc.sync.dma_start(out=c_raw, in_=centers.rearrange("(q t) i -> q t i", t=PACK))
+
+        v = const.tile([P, PACK], F32, name="v")
+        nc.vector.tensor_copy(out=v, in_=graw)
+        nabs = const.tile([P, PACK], F32, name="nabs")
+        nc.vector.scalar_tensor_tensor(out=nabs, in0=v, scalar=-1.0, in1=v, op0=ALU.mult, op1=ALU.min)
+        en = const.tile([P, PACK], F32, name="en")
+        nc.scalar.activation(out=en, in_=nabs, func=ACT.Exp)
+        l1p = const.tile([P, PACK], F32, name="l1p")
+        nc.scalar.activation(out=l1p, in_=en, func=ACT.Ln, bias=1.0)
+        gam = const.tile([P, PACK], F32, name="gam")
+        nc.vector.scalar_tensor_tensor(out=gam, in0=v, scalar=0.0, in1=l1p, op0=ALU.max, op1=ALU.add)
+        neg_g = const.tile([P, PACK], F32, name="neg_g")
+        nc.vector.tensor_scalar_mul(out=neg_g, in0=gam, scalar1=-1.0)
+        m2g = const.tile([P, PACK], F32, name="m2g")
+        nc.vector.tensor_scalar_mul(out=m2g, in0=gam, scalar1=-2.0)
+
+        su_part = const.tile([P, G * PACK], F32, name="su_part")
+        sb_part = const.tile([P, G * PACK], F32, name="sb_part")
+
+        c_in = const.tile([P, D, PACK], BF16, name="c_in", align_bytes=64)
+        nc.vector.tensor_copy(out=c_in, in_=c_raw.rearrange("q t i -> q i t"))
+        ccodes = const.tile([P, D], U32, name="ccodes", align_bytes=64)
+        csc = const.tile([P, D], U8, name="csc", align_bytes=64)
+        nc.vector.quantize_mx(out=ccodes.bitcast(E4X4), scales=csc, in_=c_in.rearrange("q i t -> q (i t)"))
+
+        tcodes = const.tile([P, G, U], U32, name="tcodes", align_bytes=64)
+        tsc = const.tile([P, G, U], U8, name="tsc", align_bytes=64)
+        xcodes = const.tile([P, G, D], U32, name="xcodes", align_bytes=64)
+        xsc = const.tile([P, G, D], U8, name="xsc", align_bytes=64)
+
+        dz32_t = []
+        dzk_t = []
+
+        def stage_a(g):
+            d2_g = d2_t[g]
+            go_g = go_t[g]
+            gm = work.tile([P, PACK, U], BF16, name="gm")
+            nc.vector.scalar_tensor_tensor(
+                out=gm.rearrange("p j u -> p (j u)"),
+                in0=d2_g.rearrange("p j u -> p (j u)"),
+                scalar=0.0,
+                in1=go_g.rearrange("p j u -> p (j u)"),
+                op0=ALU.is_gt,
+                op1=ALU.mult,
+            )
+            e = work.tile([P, PACK, GT], F32, name="e")
+            for t in range(PACK):
+                ps = psum.tile([P, GT], F32, name="d2T", tag="d2T")
+                for j in range(PACK):
+                    nc.tensor.transpose(ps[:, j * P : (j + 1) * P], d2_g[:, j, t::PACK], ident)
+                nc.scalar.activation(out=e[:, t, :], in_=ps, func=ACT.Exp, scale=neg_g[:, t : t + 1])
+            words = gm.bitcast(F32)
+            dz32 = work.tile([P, PACK, GT], F32, name="dz32")
+            for h in range(2):
+                ps = psum.tile([P, GT], F32, name="gmT", tag="gmT")
+                for j in range(PACK):
+                    nc.tensor.transpose(ps[:, j * P : (j + 1) * P], words[:, j, h::2], ident)
+                pv = ps.bitcast(BF16).rearrange("q (c s) -> q c s", s=2)
+                for s in range(2):
+                    t = 2 * h + s
+                    nc.vector.scalar_tensor_tensor(
+                        out=dz32[:, t, :],
+                        in0=pv[:, :, s],
+                        scalar=m2g[:, t : t + 1],
+                        in1=e[:, t, :],
+                        op0=ALU.mult,
+                        op1=ALU.mult,
+                        accum_out=su_part[:, g * PACK + t : g * PACK + t + 1],
+                    )
+            dz32_t.append(dz32)
+
+        def stage_b(g):
+            dz32 = dz32_t[g]
+            x_g = x_t[g]
+            qf_in = work.tile([P, GT, PACK], BF16, name="qf_in", align_bytes=64)
+            nc.vector.tensor_copy(out=qf_in, in_=dz32.rearrange("q t c -> q c t"))
+            fcodes = work.tile([P, GT], U32, name="fcodes", align_bytes=64)
+            fsc = work.tile([P, GT], U8, name="fsc", align_bytes=64)
+            nc.vector.quantize_mx(out=fcodes.bitcast(E5X4), scales=fsc, in_=qf_in.rearrange("q c t -> q (c t)"))
+            dzk = work.tile([P, PACK, U], BF16, name="dzk")
+            for j in range(PACK):
+                ps = psum.tile([P, U], F32, name="dzB", tag="dzB")
+                for t in range(PACK):
+                    nc.tensor.transpose(ps[:, t * P : (t + 1) * P], dz32[:, t, j * P : (j + 1) * P], ident)
+                nc.scalar.activation(
+                    out=dzk[:, j, :], in_=ps, func=ACT.Copy, accum_out=sb_part[:, g * PACK + j : g * PACK + j + 1]
+                )
+            dzk_t.append(dzk)
+            o0 = outp.tile([P, PACK, D], F32, name="o0")
+            for j in range(PACK):
+                ps = psum.tile([P, D], F32, name="px", tag="px")
+                nc.tensor.matmul_mx(
+                    out=ps,
+                    lhsT=fcodes[:, j * P : (j + 1) * P].bitcast(E5X4),
+                    lhsT_scale=fsc[:, j * P : (j + 1) * P],
+                    rhs=ccodes.bitcast(E4X4),
+                    rhs_scale=csc,
+                    start=True,
+                    stop=True,
+                )
+                nc.vector.scalar_tensor_tensor(
+                    out=o0[:, j, :],
+                    in0=x_g[:, j, :],
+                    scalar=sb_part[:, g * PACK + j : g * PACK + j + 1],
+                    in1=ps,
+                    op0=ALU.mult,
+                    op1=ALU.subtract,
+                )
+            nc.gpsimd.dma_start(out=o0_v[g], in_=o0)
+
+        def stage_c(g):
+            qt_in = work.tile([P, U, PACK], BF16, name="qt_in", align_bytes=64)
+            nc.scalar.copy(out=qt_in, in_=dzk_t[g].rearrange("p j u -> p u j"))
+            nc.vector.quantize_mx(
+                out=tcodes[:, g, :].bitcast(E5X4), scales=tsc[:, g, :], in_=qt_in.rearrange("p u j -> p (u j)")
+            )
+            qx_in = work.tile([P, D, PACK], BF16, name="qx_in", align_bytes=64)
+            nc.scalar.copy(out=qx_in, in_=x_t[g].rearrange("p j i -> p i j"))
+            nc.vector.quantize_mx(
+                out=xcodes[:, g, :].bitcast(E4X4), scales=xsc[:, g, :], in_=qx_in.rearrange("p i j -> p (i j)")
+            )
+
+        acc = []
+
+        def mx1(g):
+            for t in range(PACK):
+                nc.tensor.matmul_mx(
+                    out=acc[t],
+                    lhsT=tcodes[:, g, t * P : (t + 1) * P].bitcast(E5X4),
+                    lhsT_scale=tsc[:, g, t * P : (t + 1) * P],
+                    rhs=xcodes[:, g, :].bitcast(E4X4),
+                    rhs_scale=xsc[:, g, :],
+                    start=(g == 0),
+                    stop=(g == G - 1),
+                )
+
+        load_dz_inputs(1)
+        load_x(0)
+        for step in range(G + 2):
+            if step + 2 < G:
+                load_dz_inputs(step + 2)
+            if step + 1 < G:
+                load_x(step + 1)
+            if step < G:
+                stage_a(step)
+            if 1 <= step <= G:
+                stage_b(step - 1)
+            if step >= 2:
+                stage_c(step - 2)
+            if step == G - 1:
+                for t in range(PACK):
+                    acc_t = psum.tile([P, D], F32, name="acc%d" % t, tag=("d2T" if t < 2 else "gmT"))
+                    acc.append(acc_t)
+                for g in range(G - 2):
+                    mx1(g)
+            if step >= G:
+                mx1(step - 2)
+
+        su = const.tile([P, PACK], F32, name="su")
+        nc.vector.tensor_reduce(
+            out=su, in_=su_part.rearrange("q (g t) -> q t g", t=PACK), axis=mybir.AxisListType.X, op=ALU.add
+        )
+        o1 = const.tile([P, PACK, D], F32, name="o1")
+        for t in range(PACK):
+            nc.vector.scalar_tensor_tensor(
+                out=o1[:, t, :],
+                in0=c_raw[:, t, :],
+                scalar=su[:, t : t + 1],
+                in1=acc[t],
+                op0=ALU.mult,
+                op1=ALU.subtract,
+            )
+        nc.sync.dma_start(out=o1_v, in_=o1)

@@ -20,6 +20,12 @@ PACK = 4
 GT = P * PACK
 G = B // GT
 
+X1_ENG = "s"
+X2_ENG = "g"
+X3_ENG = "g"
+LAST_ON_V = True
+CHUNKS = 4
+
 
 def tile_rbflayer_v_kernel(tc, x, centers, gamma_raw, d2, grad_out, out_0, out_1):
     nc = tc.nc
@@ -28,6 +34,24 @@ def tile_rbflayer_v_kernel(tc, x, centers, gamma_raw, d2, grad_out, out_0, out_1
     x_v = x.rearrange("(g p j) i -> g p j i", p=P, j=PACK)
     o0_v = out_0.rearrange("(g p j) i -> g p j i", p=P, j=PACK)
     o1_v = out_1.rearrange("(q t) i -> q t i", t=PACK)
+
+    def interleave(eng, dst, src):
+        n = dst.shape[1]
+        if eng == "v":
+            nc.vector.tensor_copy(out=dst, in_=src.rearrange("p j n -> p n j"))
+        elif eng == "s":
+            nc.scalar.copy(out=dst, in_=src.rearrange("p j n -> p n j"))
+        else:
+            w = n // CHUNKS
+            for c in range(CHUNKS):
+                nc.gpsimd.tensor_scalar(
+                    out=dst[:, c * w : (c + 1) * w, :],
+                    in0=src[:, :, c * w : (c + 1) * w].rearrange("p j n -> p n j"),
+                    scalar1=1.0,
+                    scalar2=0.0,
+                    op0=ALU.mult,
+                    op1=ALU.add,
+                )
 
     with ExitStack() as ctx:
         const = ctx.enter_context(tc.tile_pool(name="const", bufs=1))
@@ -45,15 +69,15 @@ def tile_rbflayer_v_kernel(tc, x, centers, gamma_raw, d2, grad_out, out_0, out_1
         go_t = []
         x_t = []
 
-        def load_dz_inputs(g):
+        def load_group(g):
             d2_g = ld3.tile([P, PACK, U], F32, name="d2_g")
             nc.sync.dma_start(out=d2_g, in_=d2_v[g])
             go_g = ld3.tile([P, PACK, U], BF16, name="go_g")
             nc.sync.dma_start(out=go_g, in_=go_v[g])
             d2_t.append(d2_g)
             go_t.append(go_g)
-
-        def load_x(g):
+            if g == 0:
+                nc.sync.dma_start(out=c_raw, in_=centers.rearrange("(q t) i -> q t i", t=PACK))
             x_g = ld4.tile([P, PACK, D], BF16, name="x_g")
             nc.sync.dma_start(out=x_g, in_=x_v[g])
             x_t.append(x_g)
@@ -64,8 +88,8 @@ def tile_rbflayer_v_kernel(tc, x, centers, gamma_raw, d2, grad_out, out_0, out_1
         ident = const.tile([P, P], F32, name="ident")
         make_identity(nc, ident)
 
-        load_dz_inputs(0)
-        nc.sync.dma_start(out=c_raw, in_=centers.rearrange("(q t) i -> q t i", t=PACK))
+        load_group(0)
+        load_group(1)
 
         v = const.tile([P, PACK], F32, name="v")
         nc.vector.tensor_copy(out=v, in_=graw)
@@ -99,28 +123,29 @@ def tile_rbflayer_v_kernel(tc, x, centers, gamma_raw, d2, grad_out, out_0, out_1
         dz32_t = []
         dzk_t = []
 
+        def stage_x(g):
+            qx_in = work.tile([P, D, PACK], BF16, name="qx_in", align_bytes=64)
+            interleave(X3_ENG, qx_in, x_t[g])
+            nc.vector.quantize_mx(
+                out=xcodes[:, g, :].bitcast(E4X4), scales=xsc[:, g, :], in_=qx_in.rearrange("p i j -> p (i j)")
+            )
+
         def stage_a(g):
             d2_g = d2_t[g]
-            go_g = go_t[g]
-            gm = work.tile([P, PACK, U], BF16, name="gm")
-            nc.vector.scalar_tensor_tensor(
-                out=gm.rearrange("p j u -> p (j u)"),
-                in0=d2_g.rearrange("p j u -> p (j u)"),
-                scalar=0.0,
-                in1=go_g.rearrange("p j u -> p (j u)"),
-                op0=ALU.is_gt,
-                op1=ALU.mult,
-            )
-            e = work.tile([P, PACK, GT], F32, name="e")
+            em = work.tile([P, PACK, GT], F32, name="em")
             for t in range(PACK):
                 ps = psum.tile([P, GT], F32, name="d2T", tag="d2T")
                 for j in range(PACK):
                     nc.tensor.transpose(ps[:, j * P : (j + 1) * P], d2_g[:, j, t::PACK], ident)
-                nc.scalar.activation(out=e[:, t, :], in_=ps, func=ACT.Exp, scale=neg_g[:, t : t + 1])
-            words = gm.bitcast(F32)
+                e = outp.tile([P, GT], F32, name="e")
+                nc.scalar.activation(out=e, in_=ps, func=ACT.Exp, scale=neg_g[:, t : t + 1])
+                nc.vector.scalar_tensor_tensor(
+                    out=em[:, t, :], in0=ps, scalar=0.0, in1=e, op0=ALU.is_gt, op1=ALU.mult
+                )
+            words = go_t[g].bitcast(F32)
             dz32 = work.tile([P, PACK, GT], F32, name="dz32")
             for h in range(2):
-                ps = psum.tile([P, GT], F32, name="gmT", tag="gmT")
+                ps = psum.tile([P, GT], F32, name="goT", tag="goT")
                 for j in range(PACK):
                     nc.tensor.transpose(ps[:, j * P : (j + 1) * P], words[:, j, h::2], ident)
                 pv = ps.bitcast(BF16).rearrange("q (c s) -> q c s", s=2)
@@ -130,7 +155,7 @@ def tile_rbflayer_v_kernel(tc, x, centers, gamma_raw, d2, grad_out, out_0, out_1
                         out=dz32[:, t, :],
                         in0=pv[:, :, s],
                         scalar=m2g[:, t : t + 1],
-                        in1=e[:, t, :],
+                        in1=em[:, t, :],
                         op0=ALU.mult,
                         op1=ALU.mult,
                         accum_out=su_part[:, g * PACK + t : g * PACK + t + 1],
@@ -138,10 +163,11 @@ def tile_rbflayer_v_kernel(tc, x, centers, gamma_raw, d2, grad_out, out_0, out_1
             dz32_t.append(dz32)
 
         def stage_b(g):
+            last = LAST_ON_V and g == G - 1
             dz32 = dz32_t[g]
             x_g = x_t[g]
             qf_in = work.tile([P, GT, PACK], BF16, name="qf_in", align_bytes=64)
-            nc.vector.tensor_copy(out=qf_in, in_=dz32.rearrange("q t c -> q c t"))
+            interleave("v" if last else X1_ENG, qf_in, dz32)
             fcodes = work.tile([P, GT], U32, name="fcodes", align_bytes=64)
             fsc = work.tile([P, GT], U8, name="fsc", align_bytes=64)
             nc.vector.quantize_mx(out=fcodes.bitcast(E5X4), scales=fsc, in_=qf_in.rearrange("q c t -> q (c t)"))
@@ -174,18 +200,17 @@ def tile_rbflayer_v_kernel(tc, x, centers, gamma_raw, d2, grad_out, out_0, out_1
                     op0=ALU.mult,
                     op1=ALU.subtract,
                 )
-            nc.gpsimd.dma_start(out=o0_v[g], in_=o0)
+                if g == G - 1:
+                    nc.sync.dma_start(out=o0_v[g][:, j, :], in_=o0[:, j, :])
+            if g < G - 1:
+                nc.sync.dma_start(out=o0_v[g], in_=o0)
 
         def stage_c(g):
+            last = LAST_ON_V and g == G - 1
             qt_in = work.tile([P, U, PACK], BF16, name="qt_in", align_bytes=64)
-            nc.scalar.copy(out=qt_in, in_=dzk_t[g].rearrange("p j u -> p u j"))
+            interleave("v" if last else X2_ENG, qt_in, dzk_t[g])
             nc.vector.quantize_mx(
                 out=tcodes[:, g, :].bitcast(E5X4), scales=tsc[:, g, :], in_=qt_in.rearrange("p u j -> p (u j)")
-            )
-            qx_in = work.tile([P, D, PACK], BF16, name="qx_in", align_bytes=64)
-            nc.scalar.copy(out=qx_in, in_=x_t[g].rearrange("p j i -> p i j"))
-            nc.vector.quantize_mx(
-                out=xcodes[:, g, :].bitcast(E4X4), scales=xsc[:, g, :], in_=qx_in.rearrange("p i j -> p (i j)")
             )
 
         acc = []
@@ -202,22 +227,19 @@ def tile_rbflayer_v_kernel(tc, x, centers, gamma_raw, d2, grad_out, out_0, out_1
                     stop=(g == G - 1),
                 )
 
-        load_dz_inputs(1)
-        load_x(0)
         for step in range(G + 2):
             if step + 2 < G:
-                load_dz_inputs(step + 2)
-            if step + 1 < G:
-                load_x(step + 1)
+                load_group(step + 2)
             if step < G:
                 stage_a(step)
+                stage_x(step)
             if 1 <= step <= G:
                 stage_b(step - 1)
             if step >= 2:
                 stage_c(step - 2)
             if step == G - 1:
                 for t in range(PACK):
-                    acc_t = psum.tile([P, D], F32, name="acc%d" % t, tag=("d2T" if t < 2 else "gmT"))
+                    acc_t = psum.tile([P, D], F32, name="acc%d" % t, tag=("d2T" if t < 2 else "goT"))
                     acc.append(acc_t)
                 for g in range(G - 2):
                     mx1(g)
@@ -238,4 +260,4 @@ def tile_rbflayer_v_kernel(tc, x, centers, gamma_raw, d2, grad_out, out_0, out_1
                 op0=ALU.mult,
                 op1=ALU.subtract,
             )
-        nc.sync.dma_start(out=o1_v, in_=o1)
+            nc.sync.dma_start(out=o1_v[:, t, :], in_=o1[:, t, :])

@@ -19,12 +19,13 @@ P = 128
 PACK = 4
 GT = P * PACK
 G = B // GT
+NA = U // P
+NK = G * NA
+HALF = GT // 2
 
-X1_ENG = "s"
 X2_ENG = "g"
 X3_ENG = "g"
-LAST_ON_V = True
-CHUNKS = 4
+MANUAL = True
 
 
 def tile_rbflayer_v_kernel(tc, x, centers, gamma_raw, d2, grad_out, out_0, out_1):
@@ -33,81 +34,75 @@ def tile_rbflayer_v_kernel(tc, x, centers, gamma_raw, d2, grad_out, out_0, out_1
     go_v = grad_out.rearrange("(g p j) u -> g p j u", p=P, j=PACK)
     x_v = x.rearrange("(g p j) i -> g p j i", p=P, j=PACK)
     o0_v = out_0.rearrange("(g p j) i -> g p j i", p=P, j=PACK)
-    o1_v = out_1.rearrange("(q t) i -> q t i", t=PACK)
+    o1_v = out_1.rearrange("(a m) i -> m a i", m=P)
 
-    def interleave(eng, dst, src):
-        n = dst.shape[1]
+    def interleave(eng, dst, src, lo, hi):
+        d = dst[:, lo:hi, :]
+        s = src[:, :, lo:hi].rearrange("p j n -> p n j")
         if eng == "v":
-            nc.vector.tensor_copy(out=dst, in_=src.rearrange("p j n -> p n j"))
+            nc.vector.tensor_copy(out=d, in_=s)
         elif eng == "s":
-            nc.scalar.copy(out=dst, in_=src.rearrange("p j n -> p n j"))
+            nc.scalar.copy(out=d, in_=s)
         else:
-            w = n // CHUNKS
-            for c in range(CHUNKS):
-                nc.gpsimd.tensor_scalar(
-                    out=dst[:, c * w : (c + 1) * w, :],
-                    in0=src[:, :, c * w : (c + 1) * w].rearrange("p j n -> p n j"),
-                    scalar1=1.0,
-                    scalar2=0.0,
-                    op0=ALU.mult,
-                    op1=ALU.add,
-                )
+            nc.gpsimd.tensor_scalar(out=d, in0=s, scalar1=1.0, scalar2=0.0, op0=ALU.mult, op1=ALU.add)
 
     with ExitStack() as ctx:
         const = ctx.enter_context(tc.tile_pool(name="const", bufs=1))
         ld3 = ctx.enter_context(tc.tile_pool(name="ld3", bufs=3))
-        ld4 = ctx.enter_context(tc.tile_pool(name="ld4", bufs=4))
+        ld6 = ctx.enter_context(tc.tile_pool(name="ld6", bufs=G))
         work = ctx.enter_context(tc.tile_pool(name="work", bufs=2))
-        outp = ctx.enter_context(tc.tile_pool(name="outp", bufs=3))
+        work3 = ctx.enter_context(tc.tile_pool(name="work3", bufs=3))
         psum = ctx.enter_context(tc.psum_pool(name="psum", bufs=2))
+        if MANUAL:
+            ctx.enter_context(tc.manual_schedule())
 
-        graw = const.tile([P, PACK], BF16, name="graw")
-        nc.sync.dma_start(out=graw, in_=gamma_raw.rearrange("(q t) -> q t", t=PACK))
+        d2_t = {}
+        go_t = {}
+        x_t = {}
+
+        def load_dz(g):
+            d2_t[g] = ld3.tile([P, PACK, U], F32, name="d2_g")
+            nc.sync.dma_start(out=d2_t[g], in_=d2_v[g])
+            go_t[g] = ld3.tile([P, PACK, U], BF16, name="go_g")
+            nc.sync.dma_start(out=go_t[g], in_=go_v[g])
+
+        def load_x(g):
+            x_t[g] = ld6.tile([P, PACK, D], BF16, name="x_g")
+            nc.sync.dma_start(out=x_t[g], in_=x_v[g])
+
+        graw = const.tile([P, NA], BF16, name="graw")
+        with nc.allow_non_contiguous_dma(reason="512 two-byte values, once, at the start"):
+            nc.scalar.dma_start(out=graw, in_=gamma_raw.rearrange("(a m) -> m a", m=P))
         c_raw = const.tile([P, PACK, D], BF16, name="c_raw")
-
-        d2_t = []
-        go_t = []
-        x_t = []
-
-        def load_group(g):
-            d2_g = ld3.tile([P, PACK, U], F32, name="d2_g")
-            nc.sync.dma_start(out=d2_g, in_=d2_v[g])
-            go_g = ld3.tile([P, PACK, U], BF16, name="go_g")
-            nc.sync.dma_start(out=go_g, in_=go_v[g])
-            d2_t.append(d2_g)
-            go_t.append(go_g)
-            if g == 0:
-                nc.sync.dma_start(out=c_raw, in_=centers.rearrange("(q t) i -> q t i", t=PACK))
-            x_g = ld4.tile([P, PACK, D], BF16, name="x_g")
-            nc.sync.dma_start(out=x_g, in_=x_v[g])
-            x_t.append(x_g)
+        nc.sync.dma_start(out=c_raw, in_=centers.rearrange("(q t) i -> q t i", t=PACK))
+        load_dz(0)
+        load_x(0)
+        load_dz(1)
+        load_x(1)
+        load_dz(2)
+        load_x(2)
+        c_am = const.tile([P, NA, D], BF16, name="c_am")
+        nc.sync.dma_start(out=c_am, in_=centers.rearrange("(a m) i -> m a i", m=P))
+        load_x(3)
+        load_x(4)
+        load_x(5)
 
         warm = const.tile([P, 1], F32, name="warm")
         nc.vector.memset(warm, 0.0)
         nc.scalar.activation(out=warm, in_=warm, func=ACT.Exp)
         ident = const.tile([P, P], F32, name="ident")
         make_identity(nc, ident)
+        ident_b = const.tile([P, P], BF16, name="ident_b")
+        make_identity(nc, ident_b)
 
-        load_group(0)
-        load_group(1)
-
-        v = const.tile([P, PACK], F32, name="v")
+        v = const.tile([P, NA], F32, name="v")
         nc.vector.tensor_copy(out=v, in_=graw)
-        nabs = const.tile([P, PACK], F32, name="nabs")
+        nabs = const.tile([P, NA], F32, name="nabs")
         nc.vector.scalar_tensor_tensor(out=nabs, in0=v, scalar=-1.0, in1=v, op0=ALU.mult, op1=ALU.min)
-        en = const.tile([P, PACK], F32, name="en")
+        en = const.tile([P, NA], F32, name="en")
         nc.scalar.activation(out=en, in_=nabs, func=ACT.Exp)
-        l1p = const.tile([P, PACK], F32, name="l1p")
+        l1p = const.tile([P, NA], F32, name="l1p")
         nc.scalar.activation(out=l1p, in_=en, func=ACT.Ln, bias=1.0)
-        gam = const.tile([P, PACK], F32, name="gam")
-        nc.vector.scalar_tensor_tensor(out=gam, in0=v, scalar=0.0, in1=l1p, op0=ALU.max, op1=ALU.add)
-        neg_g = const.tile([P, PACK], F32, name="neg_g")
-        nc.vector.tensor_scalar_mul(out=neg_g, in0=gam, scalar1=-1.0)
-        m2g = const.tile([P, PACK], F32, name="m2g")
-        nc.vector.tensor_scalar_mul(out=m2g, in0=gam, scalar1=-2.0)
-
-        su_part = const.tile([P, G * PACK], F32, name="su_part")
-        sb_part = const.tile([P, G * PACK], F32, name="sb_part")
 
         c_in = const.tile([P, D, PACK], BF16, name="c_in", align_bytes=64)
         nc.vector.tensor_copy(out=c_in, in_=c_raw.rearrange("q t i -> q i t"))
@@ -115,149 +110,263 @@ def tile_rbflayer_v_kernel(tc, x, centers, gamma_raw, d2, grad_out, out_0, out_1
         csc = const.tile([P, D], U8, name="csc", align_bytes=64)
         nc.vector.quantize_mx(out=ccodes.bitcast(E4X4), scales=csc, in_=c_in.rearrange("q i t -> q (i t)"))
 
+        gam = const.tile([P, NA], F32, name="gam")
+        nc.vector.scalar_tensor_tensor(out=gam, in0=v, scalar=0.0, in1=l1p, op0=ALU.max, op1=ALU.add)
+        neg_g = const.tile([P, NA], F32, name="neg_g")
+        nc.vector.tensor_scalar_mul(out=neg_g, in0=gam, scalar1=-1.0)
+        m2g = const.tile([P, NA], F32, name="m2g")
+        nc.vector.tensor_scalar_mul(out=m2g, in0=gam, scalar1=-2.0)
+
+        su_part = const.tile([P, NK], F32, name="su_part")
+        sb_part = const.tile([P, G * PACK], F32, name="sb_part")
         tcodes = const.tile([P, G, U], U32, name="tcodes", align_bytes=64)
         tsc = const.tile([P, G, U], U8, name="tsc", align_bytes=64)
         xcodes = const.tile([P, G, D], U32, name="xcodes", align_bytes=64)
         xsc = const.tile([P, G, D], U8, name="xsc", align_bytes=64)
 
-        dz32_t = []
-        dzk_t = []
-
-        def stage_x(g):
-            qx_in = work.tile([P, D, PACK], BF16, name="qx_in", align_bytes=64)
-            interleave(X3_ENG, qx_in, x_t[g])
-            nc.vector.quantize_mx(
-                out=xcodes[:, g, :].bitcast(E4X4), scales=xsc[:, g, :], in_=qx_in.rearrange("p i j -> p (i j)")
-            )
-
-        def stage_a(g):
-            d2_g = d2_t[g]
-            em = work.tile([P, PACK, GT], F32, name="em")
-            for t in range(PACK):
-                ps = psum.tile([P, GT], F32, name="d2T", tag="d2T")
-                for j in range(PACK):
-                    nc.tensor.transpose(ps[:, j * P : (j + 1) * P], d2_g[:, j, t::PACK], ident)
-                e = outp.tile([P, GT], F32, name="e")
-                nc.scalar.activation(out=e, in_=ps, func=ACT.Exp, scale=neg_g[:, t : t + 1])
-                nc.vector.scalar_tensor_tensor(
-                    out=em[:, t, :], in0=ps, scalar=0.0, in1=e, op0=ALU.is_gt, op1=ALU.mult
-                )
-            words = go_t[g].bitcast(F32)
-            dz32 = work.tile([P, PACK, GT], F32, name="dz32")
-            for h in range(2):
-                ps = psum.tile([P, GT], F32, name="goT", tag="goT")
-                for j in range(PACK):
-                    nc.tensor.transpose(ps[:, j * P : (j + 1) * P], words[:, j, h::2], ident)
-                pv = ps.bitcast(BF16).rearrange("q (c s) -> q c s", s=2)
-                for s in range(2):
-                    t = 2 * h + s
-                    nc.vector.scalar_tensor_tensor(
-                        out=dz32[:, t, :],
-                        in0=pv[:, :, s],
-                        scalar=m2g[:, t : t + 1],
-                        in1=em[:, t, :],
-                        op0=ALU.mult,
-                        op1=ALU.mult,
-                        accum_out=su_part[:, g * PACK + t : g * PACK + t + 1],
-                    )
-            dz32_t.append(dz32)
-
-        def stage_b(g):
-            last = LAST_ON_V and g == G - 1
-            dz32 = dz32_t[g]
-            x_g = x_t[g]
-            qf_in = work.tile([P, GT, PACK], BF16, name="qf_in", align_bytes=64)
-            interleave("v" if last else X1_ENG, qf_in, dz32)
-            fcodes = work.tile([P, GT], U32, name="fcodes", align_bytes=64)
-            fsc = work.tile([P, GT], U8, name="fsc", align_bytes=64)
-            nc.vector.quantize_mx(out=fcodes.bitcast(E5X4), scales=fsc, in_=qf_in.rearrange("q c t -> q (c t)"))
-            dzk = work.tile([P, PACK, U], BF16, name="dzk")
-            for j in range(PACK):
-                ps = psum.tile([P, U], F32, name="dzB", tag="dzB")
-                for t in range(PACK):
-                    nc.tensor.transpose(ps[:, t * P : (t + 1) * P], dz32[:, t, j * P : (j + 1) * P], ident)
-                nc.scalar.activation(
-                    out=dzk[:, j, :], in_=ps, func=ACT.Copy, accum_out=sb_part[:, g * PACK + j : g * PACK + j + 1]
-                )
-            dzk_t.append(dzk)
-            o0 = outp.tile([P, PACK, D], F32, name="o0")
-            for j in range(PACK):
-                ps = psum.tile([P, D], F32, name="px", tag="px")
-                nc.tensor.matmul_mx(
-                    out=ps,
-                    lhsT=fcodes[:, j * P : (j + 1) * P].bitcast(E5X4),
-                    lhsT_scale=fsc[:, j * P : (j + 1) * P],
-                    rhs=ccodes.bitcast(E4X4),
-                    rhs_scale=csc,
-                    start=True,
-                    stop=True,
-                )
-                nc.vector.scalar_tensor_tensor(
-                    out=o0[:, j, :],
-                    in0=x_g[:, j, :],
-                    scalar=sb_part[:, g * PACK + j : g * PACK + j + 1],
-                    in1=ps,
-                    op0=ALU.mult,
-                    op1=ALU.subtract,
-                )
-                if g == G - 1:
-                    nc.sync.dma_start(out=o0_v[g][:, j, :], in_=o0[:, j, :])
-            if g < G - 1:
-                nc.sync.dma_start(out=o0_v[g], in_=o0)
-
-        def stage_c(g):
-            last = LAST_ON_V and g == G - 1
-            qt_in = work.tile([P, U, PACK], BF16, name="qt_in", align_bytes=64)
-            interleave("v" if last else X2_ENG, qt_in, dzk_t[g])
-            nc.vector.quantize_mx(
-                out=tcodes[:, g, :].bitcast(E5X4), scales=tsc[:, g, :], in_=qt_in.rearrange("p u j -> p (u j)")
-            )
-
+        d2T = {}
+        goT = {}
+        e_t = {}
+        em_t = {}
+        dz32_t = {}
+        dzB = {}
+        dzk_t = {}
+        wT = {}
+        qf_t = {}
+        fq_t = {}
+        px = {}
+        o0_t = {}
+        qt_t = {}
+        qx_t = {}
         acc = []
 
-        def mx1(g):
-            for t in range(PACK):
+        def op_td(k):
+            g, a = divmod(k, NA)
+            d2T[k] = psum.tile([P, GT], F32, name="d2T", tag="d2T")
+            for j in range(PACK):
+                nc.tensor.transpose(d2T[k][:, j * P : (j + 1) * P], d2_t[g][:, j, a * P : (a + 1) * P], ident)
+
+        def op_s1(k):
+            a = k % NA
+            e_t[k] = work3.tile([P, GT], F32, name="e")
+            nc.scalar.activation(out=e_t[k], in_=d2T[k], func=ACT.Exp, scale=neg_g[:, a : a + 1])
+
+        def op_tg(k):
+            g, a = divmod(k, NA)
+            goT[k] = psum.tile([P, GT], BF16, name="goT", tag="goT")
+            for j in range(PACK):
+                nc.tensor.transpose(goT[k][:, j * P : (j + 1) * P], go_t[g][:, j, a * P : (a + 1) * P], ident_b)
+
+        def op_v1(k):
+            em_t[k] = work3.tile([P, GT], F32, name="em")
+            nc.vector.scalar_tensor_tensor(
+                out=em_t[k], in0=d2T[k], scalar=0.0, in1=e_t[k], op0=ALU.is_gt, op1=ALU.mult
+            )
+
+        def op_v2(k):
+            g, a = divmod(k, NA)
+            if a == 0:
+                dz32_t[g] = work.tile([P, NA, GT], F32, name="dz32")
+            nc.vector.scalar_tensor_tensor(
+                out=dz32_t[g][:, a, :],
+                in0=goT[k],
+                scalar=m2g[:, a : a + 1],
+                in1=em_t[k],
+                op0=ALU.mult,
+                op1=ALU.mult,
+                accum_out=su_part[:, k : k + 1],
+            )
+
+        def op_tb(g, j):
+            dzB[(g, j)] = psum.tile([P, U], F32, name="dzB", tag="sB")
+            for a in range(NA):
+                nc.tensor.transpose(dzB[(g, j)][:, a * P : (a + 1) * P], dz32_t[g][:, a, j * P : (j + 1) * P], ident)
+
+        def op_s2(g, j):
+            if j == 0:
+                dzk_t[g] = work.tile([P, PACK, U], BF16, name="dzk")
+            c = g * PACK + j
+            nc.scalar.activation(out=dzk_t[g][:, j, :], in_=dzB[(g, j)], func=ACT.Copy, accum_out=sb_part[:, c : c + 1])
+
+        def op_tw(g, jp):
+            words = dzk_t[g].bitcast(F32)
+            wT[(g, jp)] = psum.tile([P, 2, HALF], F32, name="wT", tag="sB")
+            for h in range(2):
+                for jj in range(2):
+                    nc.tensor.transpose(wT[(g, jp)][:, h, jj * P : (jj + 1) * P], words[:, 2 * jp + jj, h::2], ident)
+
+        def op_ef(g, jp, eng):
+            if jp == 0:
+                qf_t[g] = work.tile([P, GT, PACK], BF16, name="qf_in", align_bytes=64)
+            qf_w = qf_t[g].rearrange("q c t -> q (c t)").bitcast(F32).rearrange("q (c h) -> q c h", h=2)
+            dst = qf_w[:, jp * HALF : (jp + 1) * HALF, :]
+            src = wT[(g, jp)].rearrange("q h c -> q c h")
+            if eng == "v":
+                nc.vector.tensor_copy(out=dst, in_=src)
+            else:
+                nc.scalar.copy(out=dst, in_=src)
+
+        def op_qf(g, jp):
+            if jp == 0:
+                fcodes = work.tile([P, GT], U32, name="fcodes", align_bytes=64)
+                fsc = work.tile([P, GT], U8, name="fsc", align_bytes=64)
+                fq_t[g] = (fcodes, fsc)
+            fcodes, fsc = fq_t[g]
+            nc.vector.quantize_mx(
+                out=fcodes[:, jp * HALF : (jp + 1) * HALF].bitcast(E5X4),
+                scales=fsc[:, jp * HALF : (jp + 1) * HALF],
+                in_=qf_t[g][:, jp * HALF : (jp + 1) * HALF, :].rearrange("q c t -> q (c t)"),
+            )
+
+        def op_m0(g, j):
+            fcodes, fsc = fq_t[g]
+            px[(g, j)] = psum.tile([P, D], F32, name="px", tag="px")
+            nc.tensor.matmul_mx(
+                out=px[(g, j)],
+                lhsT=fcodes[:, j * P : (j + 1) * P].bitcast(E5X4),
+                lhsT_scale=fsc[:, j * P : (j + 1) * P],
+                rhs=ccodes.bitcast(E4X4),
+                rhs_scale=csc,
+                start=True,
+                stop=True,
+            )
+
+        def op_e0(g, j):
+            if j == 0:
+                o0_t[g] = work.tile([P, PACK, D], F32, name="o0")
+            c = g * PACK + j
+            nc.vector.scalar_tensor_tensor(
+                out=o0_t[g][:, j, :],
+                in0=x_t[g][:, j, :],
+                scalar=sb_part[:, c : c + 1],
+                in1=px[(g, j)],
+                op0=ALU.mult,
+                op1=ALU.subtract,
+            )
+            if g == G - 1:
+                nc.sync.dma_start(out=o0_v[g][:, j, :], in_=o0_t[g][:, j, :])
+            elif j == PACK - 1:
+                nc.sync.dma_start(out=o0_v[g], in_=o0_t[g])
+
+        def op_x2(g, c0, c1, eng):
+            if c0 == 0:
+                qt_t[g] = work.tile([P, U, PACK], BF16, name="qt_in", align_bytes=64)
+            for c in range(c0, c1):
+                interleave(eng, qt_t[g], dzk_t[g], c * P, (c + 1) * P)
+
+        def op_qt(g):
+            nc.vector.quantize_mx(
+                out=tcodes[:, g, :].bitcast(E5X4), scales=tsc[:, g, :], in_=qt_t[g].rearrange("p u j -> p (u j)")
+            )
+
+        def op_x3(g, c0, c1):
+            if c0 == 0:
+                qx_t[g] = work.tile([P, D, PACK], BF16, name="qx_in", align_bytes=64)
+            for c in range(c0, c1):
+                interleave(X3_ENG, qx_t[g], x_t[g], c * P, (c + 1) * P)
+
+        def op_qx(g):
+            nc.vector.quantize_mx(
+                out=xcodes[:, g, :].bitcast(E4X4), scales=xsc[:, g, :], in_=qx_t[g].rearrange("p i j -> p (i j)")
+            )
+
+        def op_m1(g):
+            for a in range(NA):
                 nc.tensor.matmul_mx(
-                    out=acc[t],
-                    lhsT=tcodes[:, g, t * P : (t + 1) * P].bitcast(E5X4),
-                    lhsT_scale=tsc[:, g, t * P : (t + 1) * P],
+                    out=acc[a],
+                    lhsT=tcodes[:, g, a * P : (a + 1) * P].bitcast(E5X4),
+                    lhsT_scale=tsc[:, g, a * P : (a + 1) * P],
                     rhs=xcodes[:, g, :].bitcast(E4X4),
                     rhs_scale=xsc[:, g, :],
                     start=(g == 0),
                     stop=(g == G - 1),
                 )
 
-        for step in range(G + 2):
-            if step + 2 < G:
-                load_group(step + 2)
-            if step < G:
-                stage_a(step)
-                stage_x(step)
-            if 1 <= step <= G:
-                stage_b(step - 1)
-            if step >= 2:
-                stage_c(step - 2)
-            if step == G - 1:
-                for t in range(PACK):
-                    acc_t = psum.tile([P, D], F32, name="acc%d" % t, tag=("d2T" if t < 2 else "goT"))
-                    acc.append(acc_t)
-                for g in range(G - 2):
-                    mx1(g)
-            if step >= G:
-                mx1(step - 2)
+        op_x3(0, 0, PACK)
+        for n in range(-1, NK + 5):
+            if n >= 4 and n % 4 == 0 and n // 4 + 2 < G:
+                load_dz(n // 4 + 2)
+            if 0 <= n + 1 < NK:
+                op_td(n + 1)
+                op_s1(n + 1)
+            if 0 <= n < NK:
+                op_tg(n)
+                op_v1(n)
+            if 0 <= n - 1 < NK:
+                op_v2(n - 1)
+            if n == NK:
+                for a in range(NA):
+                    acc.append(psum.tile([P, D], F32, name="acc%d" % a, tag=("d2T" if a < 2 else "goT")))
+            gc, phi = divmod(n - 4, 4)
+            last = gc == G - 1
+            if 0 <= gc - 1 < G and phi == 0:
+                op_m0(gc - 1, 2)
+                op_m0(gc - 1, 3)
+                op_e0(gc - 1, 2)
+                op_e0(gc - 1, 3)
+            if 0 <= gc - 1 < G and phi == 1 and gc - 1 < G - 1:
+                op_qt(gc - 1)
+            if 0 <= gc < G:
+                if phi == 0:
+                    op_tb(gc, 0)
+                    op_s2(gc, 0)
+                    op_tb(gc, 1)
+                    op_s2(gc, 1)
+                    if gc + 1 < G:
+                        op_x3(gc + 1, 0, 2)
+                elif phi == 1:
+                    op_tb(gc, 2)
+                    op_s2(gc, 2)
+                    op_tb(gc, 3)
+                    op_s2(gc, 3)
+                    op_tw(gc, 0)
+                    op_ef(gc, 0, "v" if last else "s")
+                    if gc + 1 < G:
+                        op_x3(gc + 1, 2, 4)
+                    if last:
+                        op_m1(0)
+                elif phi == 2:
+                    op_tw(gc, 1)
+                    op_ef(gc, 1, "v" if last else "s")
+                    op_qf(gc, 0)
+                    op_m0(gc, 0)
+                    op_m0(gc, 1)
+                    if gc + 1 < G:
+                        op_qx(gc + 1)
+                    if last:
+                        op_m1(1)
+                        op_m1(2)
+                    else:
+                        op_x2(gc, 0, 2, X2_ENG)
+                else:
+                    op_qf(gc, 1)
+                    if last:
+                        qt_t[gc] = work.tile([P, U, PACK], BF16, name="qt_in", align_bytes=64)
+                        interleave("v", qt_t[gc], dzk_t[gc], 0, U)
+                    op_e0(gc, 0)
+                    op_e0(gc, 1)
+                    if last:
+                        op_qt(gc)
+                        op_m1(3)
+                        op_m1(4)
+                    else:
+                        op_x2(gc, 2, 4, X2_ENG)
+            if n == 2:
+                op_qx(0)
+        op_m1(G - 1)
 
-        su = const.tile([P, PACK], F32, name="su")
+        su = const.tile([P, NA], F32, name="su")
         nc.vector.tensor_reduce(
-            out=su, in_=su_part.rearrange("q (g t) -> q t g", t=PACK), axis=mybir.AxisListType.X, op=ALU.add
+            out=su, in_=su_part.rearrange("m (g a) -> m a g", a=NA), axis=mybir.AxisListType.X, op=ALU.add
         )
-        o1 = const.tile([P, PACK, D], F32, name="o1")
-        for t in range(PACK):
+        o1 = const.tile([P, NA, D], F32, name="o1")
+        for a in range(NA):
             nc.vector.scalar_tensor_tensor(
-                out=o1[:, t, :],
-                in0=c_raw[:, t, :],
-                scalar=su[:, t : t + 1],
-                in1=acc[t],
+                out=o1[:, a, :],
+                in0=c_am[:, a, :],
+                scalar=su[:, a : a + 1],
+                in1=acc[a],
                 op0=ALU.mult,
                 op1=ALU.subtract,
             )
-            nc.sync.dma_start(out=o1_v[:, t, :], in_=o1[:, t, :])
+            nc.sync.dma_start(out=o1_v[:, a, :], in_=o1[:, a, :])

@@ -19,13 +19,9 @@ P = 128
 PACK = 4
 GT = P * PACK
 G = B // GT
-NA = U // P
-NK = G * NA
-HALF = GT // 2
 
-X2_ENG = "g"
-X3_ENG = "g"
-MANUAL = True
+X1_SPLIT = 2
+LAST_ON_V = True
 
 
 def tile_rbflayer_v_kernel(tc, x, centers, gamma_raw, d2, grad_out, out_0, out_1):
@@ -34,7 +30,7 @@ def tile_rbflayer_v_kernel(tc, x, centers, gamma_raw, d2, grad_out, out_0, out_1
     go_v = grad_out.rearrange("(g p j) u -> g p j u", p=P, j=PACK)
     x_v = x.rearrange("(g p j) i -> g p j i", p=P, j=PACK)
     o0_v = out_0.rearrange("(g p j) i -> g p j i", p=P, j=PACK)
-    o1_v = out_1.rearrange("(a m) i -> m a i", m=P)
+    o1_v = out_1.rearrange("(q t) i -> q t i", t=PACK)
 
     def interleave(eng, dst, src, lo, hi):
         d = dst[:, lo:hi, :]
@@ -53,8 +49,6 @@ def tile_rbflayer_v_kernel(tc, x, centers, gamma_raw, d2, grad_out, out_0, out_1
         work = ctx.enter_context(tc.tile_pool(name="work", bufs=2))
         work3 = ctx.enter_context(tc.tile_pool(name="work3", bufs=3))
         psum = ctx.enter_context(tc.psum_pool(name="psum", bufs=2))
-        if MANUAL:
-            ctx.enter_context(tc.manual_schedule())
 
         d2_t = {}
         go_t = {}
@@ -66,42 +60,30 @@ def tile_rbflayer_v_kernel(tc, x, centers, gamma_raw, d2, grad_out, out_0, out_1
             go_t[g] = ld3.tile([P, PACK, U], BF16, name="go_g")
             nc.sync.dma_start(out=go_t[g], in_=go_v[g])
 
-        def load_x(g):
-            x_t[g] = ld6.tile([P, PACK, D], BF16, name="x_g")
-            nc.sync.dma_start(out=x_t[g], in_=x_v[g])
-
-        graw = const.tile([P, NA], BF16, name="graw")
-        with nc.allow_non_contiguous_dma(reason="512 two-byte values, once, at the start"):
-            nc.scalar.dma_start(out=graw, in_=gamma_raw.rearrange("(a m) -> m a", m=P))
+        graw = const.tile([P, PACK], BF16, name="graw")
+        nc.scalar.dma_start(out=graw, in_=gamma_raw.rearrange("(q t) -> q t", t=PACK))
         c_raw = const.tile([P, PACK, D], BF16, name="c_raw")
         nc.sync.dma_start(out=c_raw, in_=centers.rearrange("(q t) i -> q t i", t=PACK))
         load_dz(0)
-        load_x(0)
         load_dz(1)
-        load_x(1)
         load_dz(2)
-        load_x(2)
-        c_am = const.tile([P, NA, D], BF16, name="c_am")
-        nc.sync.dma_start(out=c_am, in_=centers.rearrange("(a m) i -> m a i", m=P))
-        load_x(3)
-        load_x(4)
-        load_x(5)
+        for g in range(G):
+            x_t[g] = ld6.tile([P, PACK, D], BF16, name="x_g")
+            nc.sync.dma_start(out=x_t[g], in_=x_v[g])
 
         warm = const.tile([P, 1], F32, name="warm")
         nc.vector.memset(warm, 0.0)
         nc.scalar.activation(out=warm, in_=warm, func=ACT.Exp)
         ident = const.tile([P, P], F32, name="ident")
         make_identity(nc, ident)
-        ident_b = const.tile([P, P], BF16, name="ident_b")
-        make_identity(nc, ident_b)
 
-        v = const.tile([P, NA], F32, name="v")
+        v = const.tile([P, PACK], F32, name="v")
         nc.vector.tensor_copy(out=v, in_=graw)
-        nabs = const.tile([P, NA], F32, name="nabs")
+        nabs = const.tile([P, PACK], F32, name="nabs")
         nc.vector.scalar_tensor_tensor(out=nabs, in0=v, scalar=-1.0, in1=v, op0=ALU.mult, op1=ALU.min)
-        en = const.tile([P, NA], F32, name="en")
+        en = const.tile([P, PACK], F32, name="en")
         nc.scalar.activation(out=en, in_=nabs, func=ACT.Exp)
-        l1p = const.tile([P, NA], F32, name="l1p")
+        l1p = const.tile([P, PACK], F32, name="l1p")
         nc.scalar.activation(out=l1p, in_=en, func=ACT.Ln, bias=1.0)
 
         c_in = const.tile([P, D, PACK], BF16, name="c_in", align_bytes=64)
@@ -110,263 +92,164 @@ def tile_rbflayer_v_kernel(tc, x, centers, gamma_raw, d2, grad_out, out_0, out_1
         csc = const.tile([P, D], U8, name="csc", align_bytes=64)
         nc.vector.quantize_mx(out=ccodes.bitcast(E4X4), scales=csc, in_=c_in.rearrange("q i t -> q (i t)"))
 
-        gam = const.tile([P, NA], F32, name="gam")
+        gam = const.tile([P, PACK], F32, name="gam")
         nc.vector.scalar_tensor_tensor(out=gam, in0=v, scalar=0.0, in1=l1p, op0=ALU.max, op1=ALU.add)
-        neg_g = const.tile([P, NA], F32, name="neg_g")
+        neg_g = const.tile([P, PACK], F32, name="neg_g")
         nc.vector.tensor_scalar_mul(out=neg_g, in0=gam, scalar1=-1.0)
-        m2g = const.tile([P, NA], F32, name="m2g")
+        m2g = const.tile([P, PACK], F32, name="m2g")
         nc.vector.tensor_scalar_mul(out=m2g, in0=gam, scalar1=-2.0)
 
-        su_part = const.tile([P, NK], F32, name="su_part")
+        su_part = const.tile([P, G * PACK], F32, name="su_part")
         sb_part = const.tile([P, G * PACK], F32, name="sb_part")
+        fcodes = const.tile([P, G, GT], U32, name="fcodes", align_bytes=64)
+        fsc = const.tile([P, G, GT], U8, name="fsc", align_bytes=64)
         tcodes = const.tile([P, G, U], U32, name="tcodes", align_bytes=64)
         tsc = const.tile([P, G, U], U8, name="tsc", align_bytes=64)
         xcodes = const.tile([P, G, D], U32, name="xcodes", align_bytes=64)
         xsc = const.tile([P, G, D], U8, name="xsc", align_bytes=64)
 
-        d2T = {}
-        goT = {}
-        e_t = {}
-        em_t = {}
         dz32_t = {}
-        dzB = {}
         dzk_t = {}
-        wT = {}
-        qf_t = {}
-        fq_t = {}
-        px = {}
-        o0_t = {}
-        qt_t = {}
-        qx_t = {}
-        acc = []
 
-        def op_td(k):
-            g, a = divmod(k, NA)
-            d2T[k] = psum.tile([P, GT], F32, name="d2T", tag="d2T")
-            for j in range(PACK):
-                nc.tensor.transpose(d2T[k][:, j * P : (j + 1) * P], d2_t[g][:, j, a * P : (a + 1) * P], ident)
-
-        def op_s1(k):
-            a = k % NA
-            e_t[k] = work3.tile([P, GT], F32, name="e")
-            nc.scalar.activation(out=e_t[k], in_=d2T[k], func=ACT.Exp, scale=neg_g[:, a : a + 1])
-
-        def op_tg(k):
-            g, a = divmod(k, NA)
-            goT[k] = psum.tile([P, GT], BF16, name="goT", tag="goT")
-            for j in range(PACK):
-                nc.tensor.transpose(goT[k][:, j * P : (j + 1) * P], go_t[g][:, j, a * P : (a + 1) * P], ident_b)
-
-        def op_v1(k):
-            em_t[k] = work3.tile([P, GT], F32, name="em")
-            nc.vector.scalar_tensor_tensor(
-                out=em_t[k], in0=d2T[k], scalar=0.0, in1=e_t[k], op0=ALU.is_gt, op1=ALU.mult
-            )
-
-        def op_v2(k):
-            g, a = divmod(k, NA)
-            if a == 0:
-                dz32_t[g] = work.tile([P, NA, GT], F32, name="dz32")
-            nc.vector.scalar_tensor_tensor(
-                out=dz32_t[g][:, a, :],
-                in0=goT[k],
-                scalar=m2g[:, a : a + 1],
-                in1=em_t[k],
-                op0=ALU.mult,
-                op1=ALU.mult,
-                accum_out=su_part[:, k : k + 1],
-            )
-
-        def op_tb(g, j):
-            dzB[(g, j)] = psum.tile([P, U], F32, name="dzB", tag="sB")
-            for a in range(NA):
-                nc.tensor.transpose(dzB[(g, j)][:, a * P : (a + 1) * P], dz32_t[g][:, a, j * P : (j + 1) * P], ident)
-
-        def op_s2(g, j):
-            if j == 0:
-                dzk_t[g] = work.tile([P, PACK, U], BF16, name="dzk")
-            c = g * PACK + j
-            nc.scalar.activation(out=dzk_t[g][:, j, :], in_=dzB[(g, j)], func=ACT.Copy, accum_out=sb_part[:, c : c + 1])
-
-        def op_tw(g, jp):
-            words = dzk_t[g].bitcast(F32)
-            wT[(g, jp)] = psum.tile([P, 2, HALF], F32, name="wT", tag="sB")
+        def stage_a(g):
+            d2_g = d2_t[g]
+            em = work.tile([P, PACK, GT], F32, name="em")
+            for t in range(PACK):
+                ps = psum.tile([P, GT], F32, name="d2T", tag="d2T", bufs=3)
+                for j in range(PACK):
+                    nc.tensor.transpose(ps[:, j * P : (j + 1) * P], d2_g[:, j, t::PACK], ident)
+                e = work3.tile([P, GT], F32, name="e")
+                nc.scalar.activation(out=e, in_=ps, func=ACT.Exp, scale=neg_g[:, t : t + 1])
+                nc.vector.scalar_tensor_tensor(
+                    out=em[:, t, :], in0=ps, scalar=0.0, in1=e, op0=ALU.is_gt, op1=ALU.mult
+                )
+            words = go_t[g].bitcast(F32)
+            dz32 = work.tile([P, PACK, GT], F32, name="dz32")
             for h in range(2):
-                for jj in range(2):
-                    nc.tensor.transpose(wT[(g, jp)][:, h, jj * P : (jj + 1) * P], words[:, 2 * jp + jj, h::2], ident)
+                ps = psum.tile([P, GT], F32, name="goT", tag="goT", bufs=2)
+                for j in range(PACK):
+                    nc.tensor.transpose(ps[:, j * P : (j + 1) * P], words[:, j, h::2], ident)
+                pv = ps.bitcast(BF16).rearrange("q (c s) -> q c s", s=2)
+                for s in range(2):
+                    t = 2 * h + s
+                    nc.vector.scalar_tensor_tensor(
+                        out=dz32[:, t, :],
+                        in0=pv[:, :, s],
+                        scalar=m2g[:, t : t + 1],
+                        in1=em[:, t, :],
+                        op0=ALU.mult,
+                        op1=ALU.mult,
+                        accum_out=su_part[:, g * PACK + t : g * PACK + t + 1],
+                    )
+            dz32_t[g] = dz32
 
-        def op_ef(g, jp, eng):
-            if jp == 0:
-                qf_t[g] = work.tile([P, GT, PACK], BF16, name="qf_in", align_bytes=64)
-            qf_w = qf_t[g].rearrange("q c t -> q (c t)").bitcast(F32).rearrange("q (c h) -> q c h", h=2)
-            dst = qf_w[:, jp * HALF : (jp + 1) * HALF, :]
-            src = wT[(g, jp)].rearrange("q h c -> q c h")
-            if eng == "v":
-                nc.vector.tensor_copy(out=dst, in_=src)
+        def stage_b(g):
+            last = LAST_ON_V and g == G - 1
+            dz32 = dz32_t[g]
+            qf_in = work.tile([P, GT, PACK], BF16, name="qf_in", align_bytes=64)
+            if last:
+                interleave("v", qf_in, dz32, 0, GT)
             else:
-                nc.scalar.copy(out=dst, in_=src)
-
-        def op_qf(g, jp):
-            if jp == 0:
-                fcodes = work.tile([P, GT], U32, name="fcodes", align_bytes=64)
-                fsc = work.tile([P, GT], U8, name="fsc", align_bytes=64)
-                fq_t[g] = (fcodes, fsc)
-            fcodes, fsc = fq_t[g]
+                for c in range(PACK):
+                    interleave("s" if c < X1_SPLIT else "g", qf_in, dz32, c * P, (c + 1) * P)
             nc.vector.quantize_mx(
-                out=fcodes[:, jp * HALF : (jp + 1) * HALF].bitcast(E5X4),
-                scales=fsc[:, jp * HALF : (jp + 1) * HALF],
-                in_=qf_t[g][:, jp * HALF : (jp + 1) * HALF, :].rearrange("q c t -> q (c t)"),
+                out=fcodes[:, g, :].bitcast(E5X4), scales=fsc[:, g, :], in_=qf_in.rearrange("q c t -> q (c t)")
             )
+            dzk = work.tile([P, PACK, U], BF16, name="dzk")
+            for j in range(PACK):
+                ps = psum.tile([P, U], F32, name="dzB", tag="dzB", bufs=3)
+                for t in range(PACK):
+                    nc.tensor.transpose(ps[:, t * P : (t + 1) * P], dz32[:, t, j * P : (j + 1) * P], ident)
+                nc.scalar.activation(
+                    out=dzk[:, j, :], in_=ps, func=ACT.Copy, accum_out=sb_part[:, g * PACK + j : g * PACK + j + 1]
+                )
+            dzk_t[g] = dzk
 
-        def op_m0(g, j):
-            fcodes, fsc = fq_t[g]
-            px[(g, j)] = psum.tile([P, D], F32, name="px", tag="px")
-            nc.tensor.matmul_mx(
-                out=px[(g, j)],
-                lhsT=fcodes[:, j * P : (j + 1) * P].bitcast(E5X4),
-                lhsT_scale=fsc[:, j * P : (j + 1) * P],
-                rhs=ccodes.bitcast(E4X4),
-                rhs_scale=csc,
-                start=True,
-                stop=True,
-            )
-
-        def op_e0(g, j):
-            if j == 0:
-                o0_t[g] = work.tile([P, PACK, D], F32, name="o0")
-            c = g * PACK + j
-            nc.vector.scalar_tensor_tensor(
-                out=o0_t[g][:, j, :],
-                in0=x_t[g][:, j, :],
-                scalar=sb_part[:, c : c + 1],
-                in1=px[(g, j)],
-                op0=ALU.mult,
-                op1=ALU.subtract,
-            )
-            if g == G - 1:
-                nc.sync.dma_start(out=o0_v[g][:, j, :], in_=o0_t[g][:, j, :])
-            elif j == PACK - 1:
-                nc.sync.dma_start(out=o0_v[g], in_=o0_t[g])
-
-        def op_x2(g, c0, c1, eng):
-            if c0 == 0:
-                qt_t[g] = work.tile([P, U, PACK], BF16, name="qt_in", align_bytes=64)
-            for c in range(c0, c1):
-                interleave(eng, qt_t[g], dzk_t[g], c * P, (c + 1) * P)
-
-        def op_qt(g):
+        def stage_c(g):
+            last = LAST_ON_V and g == G - 1
+            qt_in = work.tile([P, U, PACK], BF16, name="qt_in", align_bytes=64)
+            if last:
+                interleave("v", qt_in, dzk_t[g], 0, U)
+            else:
+                for c in range(PACK):
+                    interleave("g", qt_in, dzk_t[g], c * P, (c + 1) * P)
             nc.vector.quantize_mx(
-                out=tcodes[:, g, :].bitcast(E5X4), scales=tsc[:, g, :], in_=qt_t[g].rearrange("p u j -> p (u j)")
+                out=tcodes[:, g, :].bitcast(E5X4), scales=tsc[:, g, :], in_=qt_in.rearrange("p u j -> p (u j)")
             )
 
-        def op_x3(g, c0, c1):
-            if c0 == 0:
-                qx_t[g] = work.tile([P, D, PACK], BF16, name="qx_in", align_bytes=64)
-            for c in range(c0, c1):
-                interleave(X3_ENG, qx_t[g], x_t[g], c * P, (c + 1) * P)
+        for step in range(G + 2):
+            if 1 <= step and step + 2 < G:
+                load_dz(step + 2)
+            if step < G:
+                stage_a(step)
+            if 1 <= step <= G:
+                stage_b(step - 1)
+            if step >= 2:
+                stage_c(step - 2)
 
-        def op_qx(g):
+        for g in range(G):
+            qx_in = work.tile([P, D, PACK], BF16, name="qx_in", align_bytes=64)
+            for c in range(PACK):
+                interleave("s" if g % 2 == 0 else "g", qx_in, x_t[g], c * P, (c + 1) * P)
             nc.vector.quantize_mx(
-                out=xcodes[:, g, :].bitcast(E4X4), scales=xsc[:, g, :], in_=qx_t[g].rearrange("p i j -> p (i j)")
+                out=xcodes[:, g, :].bitcast(E4X4), scales=xsc[:, g, :], in_=qx_in.rearrange("p i j -> p (i j)")
             )
 
-        def op_m1(g):
-            for a in range(NA):
+        acc = []
+        for t in range(PACK):
+            if t < 3:
+                acc.append(psum.tile([P, D], F32, name="acc%d" % t, tag="dzB", bufs=3))
+            else:
+                acc.append(psum.tile([P, D], F32, name="acc%d" % t, tag="goT", bufs=2))
+
+        for g in range(G):
+            o0 = work3.tile([P, PACK, D], F32, name="o0")
+            for j in range(PACK):
+                ps = psum.tile([P, D], F32, name="px", tag="d2T", bufs=3)
                 nc.tensor.matmul_mx(
-                    out=acc[a],
-                    lhsT=tcodes[:, g, a * P : (a + 1) * P].bitcast(E5X4),
-                    lhsT_scale=tsc[:, g, a * P : (a + 1) * P],
+                    out=ps,
+                    lhsT=fcodes[:, g, j * P : (j + 1) * P].bitcast(E5X4),
+                    lhsT_scale=fsc[:, g, j * P : (j + 1) * P],
+                    rhs=ccodes.bitcast(E4X4),
+                    rhs_scale=csc,
+                    start=True,
+                    stop=True,
+                )
+                nc.vector.scalar_tensor_tensor(
+                    out=o0[:, j, :],
+                    in0=x_t[g][:, j, :],
+                    scalar=sb_part[:, g * PACK + j : g * PACK + j + 1],
+                    in1=ps,
+                    op0=ALU.mult,
+                    op1=ALU.subtract,
+                )
+                if g == G - 1:
+                    nc.sync.dma_start(out=o0_v[g][:, j, :], in_=o0[:, j, :])
+            if g < G - 1:
+                nc.sync.dma_start(out=o0_v[g], in_=o0)
+            for t in range(PACK):
+                nc.tensor.matmul_mx(
+                    out=acc[t],
+                    lhsT=tcodes[:, g, t * P : (t + 1) * P].bitcast(E5X4),
+                    lhsT_scale=tsc[:, g, t * P : (t + 1) * P],
                     rhs=xcodes[:, g, :].bitcast(E4X4),
                     rhs_scale=xsc[:, g, :],
                     start=(g == 0),
                     stop=(g == G - 1),
                 )
 
-        op_x3(0, 0, PACK)
-        for n in range(-1, NK + 5):
-            if n >= 4 and n % 4 == 0 and n // 4 + 2 < G:
-                load_dz(n // 4 + 2)
-            if 0 <= n + 1 < NK:
-                op_td(n + 1)
-                op_s1(n + 1)
-            if 0 <= n < NK:
-                op_tg(n)
-                op_v1(n)
-            if 0 <= n - 1 < NK:
-                op_v2(n - 1)
-            if n == NK:
-                for a in range(NA):
-                    acc.append(psum.tile([P, D], F32, name="acc%d" % a, tag=("d2T" if a < 2 else "goT")))
-            gc, phi = divmod(n - 4, 4)
-            last = gc == G - 1
-            if 0 <= gc - 1 < G and phi == 0:
-                op_m0(gc - 1, 2)
-                op_m0(gc - 1, 3)
-                op_e0(gc - 1, 2)
-                op_e0(gc - 1, 3)
-            if 0 <= gc - 1 < G and phi == 1 and gc - 1 < G - 1:
-                op_qt(gc - 1)
-            if 0 <= gc < G:
-                if phi == 0:
-                    op_tb(gc, 0)
-                    op_s2(gc, 0)
-                    op_tb(gc, 1)
-                    op_s2(gc, 1)
-                    if gc + 1 < G:
-                        op_x3(gc + 1, 0, 2)
-                elif phi == 1:
-                    op_tb(gc, 2)
-                    op_s2(gc, 2)
-                    op_tb(gc, 3)
-                    op_s2(gc, 3)
-                    op_tw(gc, 0)
-                    op_ef(gc, 0, "v" if last else "s")
-                    if gc + 1 < G:
-                        op_x3(gc + 1, 2, 4)
-                    if last:
-                        op_m1(0)
-                elif phi == 2:
-                    op_tw(gc, 1)
-                    op_ef(gc, 1, "v" if last else "s")
-                    op_qf(gc, 0)
-                    op_m0(gc, 0)
-                    op_m0(gc, 1)
-                    if gc + 1 < G:
-                        op_qx(gc + 1)
-                    if last:
-                        op_m1(1)
-                        op_m1(2)
-                    else:
-                        op_x2(gc, 0, 2, X2_ENG)
-                else:
-                    op_qf(gc, 1)
-                    if last:
-                        qt_t[gc] = work.tile([P, U, PACK], BF16, name="qt_in", align_bytes=64)
-                        interleave("v", qt_t[gc], dzk_t[gc], 0, U)
-                    op_e0(gc, 0)
-                    op_e0(gc, 1)
-                    if last:
-                        op_qt(gc)
-                        op_m1(3)
-                        op_m1(4)
-                    else:
-                        op_x2(gc, 2, 4, X2_ENG)
-            if n == 2:
-                op_qx(0)
-        op_m1(G - 1)
-
-        su = const.tile([P, NA], F32, name="su")
+        su = const.tile([P, PACK], F32, name="su")
         nc.vector.tensor_reduce(
-            out=su, in_=su_part.rearrange("m (g a) -> m a g", a=NA), axis=mybir.AxisListType.X, op=ALU.add
+            out=su, in_=su_part.rearrange("q (g t) -> q t g", t=PACK), axis=mybir.AxisListType.X, op=ALU.add
         )
-        o1 = const.tile([P, NA, D], F32, name="o1")
-        for a in range(NA):
+        o1 = const.tile([P, PACK, D], F32, name="o1")
+        for t in range(PACK):
             nc.vector.scalar_tensor_tensor(
-                out=o1[:, a, :],
-                in0=c_am[:, a, :],
-                scalar=su[:, a : a + 1],
-                in1=acc[a],
+                out=o1[:, t, :],
+                in0=c_raw[:, t, :],
+                scalar=su[:, t : t + 1],
+                in1=acc[t],
                 op0=ALU.mult,
                 op1=ALU.subtract,
             )
-            nc.sync.dma_start(out=o1_v[:, a, :], in_=o1[:, a, :])
+            nc.sync.dma_start(out=o1_v[:, t, :], in_=o1[:, t, :])

@@ -20,8 +20,11 @@ PACK = 4
 GT = P * PACK
 G = B // GT
 
-X1_SPLIT = 2
+X1_ENG = "s"
+X2_ENG = "g"
+X3_ENG = "g"
 LAST_ON_V = True
+CHUNKS = 4
 
 
 def tile_rbflayer_v_kernel(tc, x, centers, gamma_raw, d2, grad_out, out_0, out_1):
@@ -32,50 +35,66 @@ def tile_rbflayer_v_kernel(tc, x, centers, gamma_raw, d2, grad_out, out_0, out_1
     o0_v = out_0.rearrange("(g p j) i -> g p j i", p=P, j=PACK)
     o1_v = out_1.rearrange("(q t) i -> q t i", t=PACK)
 
-    def interleave(eng, dst, src, lo, hi):
-        d = dst[:, lo:hi, :]
-        s = src[:, :, lo:hi].rearrange("p j n -> p n j")
+    def interleave(eng, dst, src):
+        n = dst.shape[1]
         if eng == "v":
-            nc.vector.tensor_copy(out=d, in_=s)
+            nc.vector.tensor_copy(out=dst, in_=src.rearrange("p j n -> p n j"))
         elif eng == "s":
-            nc.scalar.copy(out=d, in_=s)
+            nc.scalar.copy(out=dst, in_=src.rearrange("p j n -> p n j"))
         else:
-            nc.gpsimd.tensor_scalar(out=d, in0=s, scalar1=1.0, scalar2=0.0, op0=ALU.mult, op1=ALU.add)
+            w = n // CHUNKS
+            for c in range(CHUNKS):
+                nc.gpsimd.tensor_scalar(
+                    out=dst[:, c * w : (c + 1) * w, :],
+                    in0=src[:, :, c * w : (c + 1) * w].rearrange("p j n -> p n j"),
+                    scalar1=1.0,
+                    scalar2=0.0,
+                    op0=ALU.mult,
+                    op1=ALU.add,
+                )
 
     with ExitStack() as ctx:
         const = ctx.enter_context(tc.tile_pool(name="const", bufs=1))
         ld3 = ctx.enter_context(tc.tile_pool(name="ld3", bufs=3))
-        ld6 = ctx.enter_context(tc.tile_pool(name="ld6", bufs=G))
+        ld4 = ctx.enter_context(tc.tile_pool(name="ld4", bufs=4))
         work = ctx.enter_context(tc.tile_pool(name="work", bufs=2))
-        work3 = ctx.enter_context(tc.tile_pool(name="work3", bufs=3))
+        outp = ctx.enter_context(tc.tile_pool(name="outp", bufs=3))
         psum = ctx.enter_context(tc.psum_pool(name="psum", bufs=2))
-
-        d2_t = {}
-        go_t = {}
-        x_t = {}
-
-        def load_dz(g):
-            d2_t[g] = ld3.tile([P, PACK, U], F32, name="d2_g")
-            nc.sync.dma_start(out=d2_t[g], in_=d2_v[g])
-            go_t[g] = ld3.tile([P, PACK, U], BF16, name="go_g")
-            nc.sync.dma_start(out=go_t[g], in_=go_v[g])
 
         graw = const.tile([P, PACK], BF16, name="graw")
         nc.scalar.dma_start(out=graw, in_=gamma_raw.rearrange("(q t) -> q t", t=PACK))
         c_raw = const.tile([P, PACK, D], BF16, name="c_raw")
-        nc.sync.dma_start(out=c_raw, in_=centers.rearrange("(q t) i -> q t i", t=PACK))
-        load_dz(0)
-        load_dz(1)
-        load_dz(2)
-        for g in range(G):
-            x_t[g] = ld6.tile([P, PACK, D], BF16, name="x_g")
-            nc.sync.dma_start(out=x_t[g], in_=x_v[g])
+
+        d2_t = []
+        go_t = []
+        x_t = []
+
+        def load_group(g):
+            d2_g = ld3.tile([P, PACK, U], F32, name="d2_g")
+            go_g = ld3.tile([P, PACK, U], BF16, name="go_g")
+            if g == 0:
+                for j in range(PACK):
+                    nc.sync.dma_start(out=d2_g[:, j, :], in_=d2_v[g][:, j, :])
+                    nc.sync.dma_start(out=go_g[:, j, :], in_=go_v[g][:, j, :])
+            else:
+                nc.sync.dma_start(out=d2_g, in_=d2_v[g])
+                nc.sync.dma_start(out=go_g, in_=go_v[g])
+            d2_t.append(d2_g)
+            go_t.append(go_g)
+            if g == 0:
+                nc.sync.dma_start(out=c_raw, in_=centers.rearrange("(q t) i -> q t i", t=PACK))
+            x_g = ld4.tile([P, PACK, D], BF16, name="x_g")
+            nc.sync.dma_start(out=x_g, in_=x_v[g])
+            x_t.append(x_g)
 
         warm = const.tile([P, 1], F32, name="warm")
         nc.vector.memset(warm, 0.0)
         nc.scalar.activation(out=warm, in_=warm, func=ACT.Exp)
         ident = const.tile([P, P], F32, name="ident")
         make_identity(nc, ident)
+
+        load_group(0)
+        load_group(1)
 
         v = const.tile([P, PACK], F32, name="v")
         nc.vector.tensor_copy(out=v, in_=graw)
@@ -85,13 +104,6 @@ def tile_rbflayer_v_kernel(tc, x, centers, gamma_raw, d2, grad_out, out_0, out_1
         nc.scalar.activation(out=en, in_=nabs, func=ACT.Exp)
         l1p = const.tile([P, PACK], F32, name="l1p")
         nc.scalar.activation(out=l1p, in_=en, func=ACT.Ln, bias=1.0)
-
-        c_in = const.tile([P, D, PACK], BF16, name="c_in", align_bytes=64)
-        nc.vector.tensor_copy(out=c_in, in_=c_raw.rearrange("q t i -> q i t"))
-        ccodes = const.tile([P, D], U32, name="ccodes", align_bytes=64)
-        csc = const.tile([P, D], U8, name="csc", align_bytes=64)
-        nc.vector.quantize_mx(out=ccodes.bitcast(E4X4), scales=csc, in_=c_in.rearrange("q i t -> q (i t)"))
-
         gam = const.tile([P, PACK], F32, name="gam")
         nc.vector.scalar_tensor_tensor(out=gam, in0=v, scalar=0.0, in1=l1p, op0=ALU.max, op1=ALU.add)
         neg_g = const.tile([P, PACK], F32, name="neg_g")
@@ -101,24 +113,41 @@ def tile_rbflayer_v_kernel(tc, x, centers, gamma_raw, d2, grad_out, out_0, out_1
 
         su_part = const.tile([P, G * PACK], F32, name="su_part")
         sb_part = const.tile([P, G * PACK], F32, name="sb_part")
-        fcodes = const.tile([P, G, GT], U32, name="fcodes", align_bytes=64)
-        fsc = const.tile([P, G, GT], U8, name="fsc", align_bytes=64)
+
+        c_in = const.tile([P, D, PACK], BF16, name="c_in", align_bytes=64)
+        nc.vector.tensor_copy(out=c_in, in_=c_raw.rearrange("q t i -> q i t"))
+        ccodes = const.tile([P, D], U32, name="ccodes", align_bytes=64)
+        csc = const.tile([P, D], U8, name="csc", align_bytes=64)
+        nc.vector.quantize_mx(out=ccodes.bitcast(E4X4), scales=csc, in_=c_in.rearrange("q i t -> q (i t)"))
+
         tcodes = const.tile([P, G, U], U32, name="tcodes", align_bytes=64)
         tsc = const.tile([P, G, U], U8, name="tsc", align_bytes=64)
         xcodes = const.tile([P, G, D], U32, name="xcodes", align_bytes=64)
         xsc = const.tile([P, G, D], U8, name="xsc", align_bytes=64)
 
-        dz32_t = {}
-        dzk_t = {}
+        dz32_t = []
+        dzk_t = []
+
+        def stage_x(g):
+            qx_in = work.tile([P, D, PACK], BF16, name="qx_in", align_bytes=64)
+            interleave(X3_ENG, qx_in, x_t[g])
+            nc.vector.quantize_mx(
+                out=xcodes[:, g, :].bitcast(E4X4), scales=xsc[:, g, :], in_=qx_in.rearrange("p i j -> p (i j)")
+            )
 
         def stage_a(g):
             d2_g = d2_t[g]
             em = work.tile([P, PACK, GT], F32, name="em")
             for t in range(PACK):
-                ps = psum.tile([P, GT], F32, name="d2T", tag="d2T", bufs=3)
+                ps = psum.tile([P, GT], F32, name="d2T", tag="d2T")
                 for j in range(PACK):
-                    nc.tensor.transpose(ps[:, j * P : (j + 1) * P], d2_g[:, j, t::PACK], ident)
-                e = work3.tile([P, GT], F32, name="e")
+                    if j < 3:
+                        nc.tensor.matmul(
+                            out=ps[:, j * P : (j + 1) * P], lhsT=d2_g[:, j, t::PACK], rhs=ident, start=True, stop=True
+                        )
+                    else:
+                        nc.tensor.transpose(ps[:, j * P : (j + 1) * P], d2_g[:, j, t::PACK], ident)
+                e = outp.tile([P, GT], F32, name="e")
                 nc.scalar.activation(out=e, in_=ps, func=ACT.Exp, scale=neg_g[:, t : t + 1])
                 nc.vector.scalar_tensor_tensor(
                     out=em[:, t, :], in0=ps, scalar=0.0, in1=e, op0=ALU.is_gt, op1=ALU.mult
@@ -126,7 +155,7 @@ def tile_rbflayer_v_kernel(tc, x, centers, gamma_raw, d2, grad_out, out_0, out_1
             words = go_t[g].bitcast(F32)
             dz32 = work.tile([P, PACK, GT], F32, name="dz32")
             for h in range(2):
-                ps = psum.tile([P, GT], F32, name="goT", tag="goT", bufs=2)
+                ps = psum.tile([P, GT], F32, name="goT", tag="goT")
                 for j in range(PACK):
                     nc.tensor.transpose(ps[:, j * P : (j + 1) * P], words[:, j, h::2], ident)
                 pv = ps.bitcast(BF16).rearrange("q (c s) -> q c s", s=2)
@@ -141,75 +170,33 @@ def tile_rbflayer_v_kernel(tc, x, centers, gamma_raw, d2, grad_out, out_0, out_1
                         op1=ALU.mult,
                         accum_out=su_part[:, g * PACK + t : g * PACK + t + 1],
                     )
-            dz32_t[g] = dz32
+            dz32_t.append(dz32)
 
         def stage_b(g):
             last = LAST_ON_V and g == G - 1
             dz32 = dz32_t[g]
+            x_g = x_t[g]
             qf_in = work.tile([P, GT, PACK], BF16, name="qf_in", align_bytes=64)
-            if last:
-                interleave("v", qf_in, dz32, 0, GT)
-            else:
-                for c in range(PACK):
-                    interleave("s" if c < X1_SPLIT else "g", qf_in, dz32, c * P, (c + 1) * P)
-            nc.vector.quantize_mx(
-                out=fcodes[:, g, :].bitcast(E5X4), scales=fsc[:, g, :], in_=qf_in.rearrange("q c t -> q (c t)")
-            )
+            interleave("v" if last else X1_ENG, qf_in, dz32)
+            fcodes = work.tile([P, GT], U32, name="fcodes", align_bytes=64)
+            fsc = work.tile([P, GT], U8, name="fsc", align_bytes=64)
+            nc.vector.quantize_mx(out=fcodes.bitcast(E5X4), scales=fsc, in_=qf_in.rearrange("q c t -> q (c t)"))
             dzk = work.tile([P, PACK, U], BF16, name="dzk")
             for j in range(PACK):
-                ps = psum.tile([P, U], F32, name="dzB", tag="dzB", bufs=3)
+                ps = psum.tile([P, U], F32, name="dzB", tag="dzB")
                 for t in range(PACK):
                     nc.tensor.transpose(ps[:, t * P : (t + 1) * P], dz32[:, t, j * P : (j + 1) * P], ident)
                 nc.scalar.activation(
                     out=dzk[:, j, :], in_=ps, func=ACT.Copy, accum_out=sb_part[:, g * PACK + j : g * PACK + j + 1]
                 )
-            dzk_t[g] = dzk
-
-        def stage_c(g):
-            last = LAST_ON_V and g == G - 1
-            qt_in = work.tile([P, U, PACK], BF16, name="qt_in", align_bytes=64)
-            if last:
-                interleave("v", qt_in, dzk_t[g], 0, U)
-            else:
-                for c in range(PACK):
-                    interleave("g", qt_in, dzk_t[g], c * P, (c + 1) * P)
-            nc.vector.quantize_mx(
-                out=tcodes[:, g, :].bitcast(E5X4), scales=tsc[:, g, :], in_=qt_in.rearrange("p u j -> p (u j)")
-            )
-
-        for step in range(G + 2):
-            if 1 <= step and step + 2 < G:
-                load_dz(step + 2)
-            if step < G:
-                stage_a(step)
-            if 1 <= step <= G:
-                stage_b(step - 1)
-            if step >= 2:
-                stage_c(step - 2)
-
-        for g in range(G):
-            qx_in = work.tile([P, D, PACK], BF16, name="qx_in", align_bytes=64)
-            for c in range(PACK):
-                interleave("s" if g % 2 == 0 else "g", qx_in, x_t[g], c * P, (c + 1) * P)
-            nc.vector.quantize_mx(
-                out=xcodes[:, g, :].bitcast(E4X4), scales=xsc[:, g, :], in_=qx_in.rearrange("p i j -> p (i j)")
-            )
-
-        acc = []
-        for t in range(PACK):
-            if t < 3:
-                acc.append(psum.tile([P, D], F32, name="acc%d" % t, tag="dzB", bufs=3))
-            else:
-                acc.append(psum.tile([P, D], F32, name="acc%d" % t, tag="goT", bufs=2))
-
-        for g in range(G):
-            o0 = work3.tile([P, PACK, D], F32, name="o0")
+            dzk_t.append(dzk)
+            o0 = outp.tile([P, PACK, D], F32, name="o0")
             for j in range(PACK):
-                ps = psum.tile([P, D], F32, name="px", tag="d2T", bufs=3)
+                ps = psum.tile([P, D], F32, name="px", tag="px")
                 nc.tensor.matmul_mx(
                     out=ps,
-                    lhsT=fcodes[:, g, j * P : (j + 1) * P].bitcast(E5X4),
-                    lhsT_scale=fsc[:, g, j * P : (j + 1) * P],
+                    lhsT=fcodes[:, j * P : (j + 1) * P].bitcast(E5X4),
+                    lhsT_scale=fsc[:, j * P : (j + 1) * P],
                     rhs=ccodes.bitcast(E4X4),
                     rhs_scale=csc,
                     start=True,
@@ -217,7 +204,7 @@ def tile_rbflayer_v_kernel(tc, x, centers, gamma_raw, d2, grad_out, out_0, out_1
                 )
                 nc.vector.scalar_tensor_tensor(
                     out=o0[:, j, :],
-                    in0=x_t[g][:, j, :],
+                    in0=x_g[:, j, :],
                     scalar=sb_part[:, g * PACK + j : g * PACK + j + 1],
                     in1=ps,
                     op0=ALU.mult,
@@ -227,6 +214,18 @@ def tile_rbflayer_v_kernel(tc, x, centers, gamma_raw, d2, grad_out, out_0, out_1
                     nc.sync.dma_start(out=o0_v[g][:, j, :], in_=o0[:, j, :])
             if g < G - 1:
                 nc.sync.dma_start(out=o0_v[g], in_=o0)
+
+        def stage_c(g):
+            last = LAST_ON_V and g == G - 1
+            qt_in = work.tile([P, U, PACK], BF16, name="qt_in", align_bytes=64)
+            interleave("v" if last else X2_ENG, qt_in, dzk_t[g])
+            nc.vector.quantize_mx(
+                out=tcodes[:, g, :].bitcast(E5X4), scales=tsc[:, g, :], in_=qt_in.rearrange("p u j -> p (u j)")
+            )
+
+        acc = []
+
+        def mx1(g):
             for t in range(PACK):
                 nc.tensor.matmul_mx(
                     out=acc[t],
@@ -237,6 +236,25 @@ def tile_rbflayer_v_kernel(tc, x, centers, gamma_raw, d2, grad_out, out_0, out_1
                     start=(g == 0),
                     stop=(g == G - 1),
                 )
+
+        for step in range(G + 2):
+            if step + 2 < G:
+                load_group(step + 2)
+            if step < G:
+                stage_a(step)
+                stage_x(step)
+            if 1 <= step <= G:
+                stage_b(step - 1)
+            if step >= 2:
+                stage_c(step - 2)
+            if step == G - 1:
+                for t in range(PACK):
+                    acc_t = psum.tile([P, D], F32, name="acc%d" % t, tag=("d2T" if t < 2 else "goT"))
+                    acc.append(acc_t)
+                for g in range(G - 2):
+                    mx1(g)
+            if step >= G:
+                mx1(step - 2)
 
         su = const.tile([P, PACK], F32, name="su")
         nc.vector.tensor_reduce(

from contextlib import ExitStack

import concourse.mybir as mybir
from concourse.masks import make_identity

B, D, U = 3072, 512, 512
FLOPS = 2 * 2 * B * U * D

F32 = mybir.dt.float32
BF16 = mybir.dt.bfloat16
U32 = mybir.dt.uint32
U8 = mybir.dt.uint8
E5X4 = mybir.dt.float8_e5m2_x4
E4X4 = mybir.dt.float8_e4m3fn_x4
ALU = mybir.AluOpType
ACT = mybir.ActivationFunctionType

P = 128
PACK = 4
GT = P * PACK
G = B // GT

X1_ENG = "s"
X2_ENG = "g"
X3_ENG = "g"
LAST_ON_V = True
CHUNKS = 4


def tile_rbflayer_v_kernel(tc, x, centers, gamma_raw, d2, grad_out, out_0, out_1):
    nc = tc.nc
    d2_v = d2.rearrange("(g p j) u -> g p j u", p=P, j=PACK)
    go_v = grad_out.rearrange("(g p j) u -> g p j u", p=P, j=PACK)
    x_v = x.rearrange("(g p j) i -> g p j i", p=P, j=PACK)
    o0_v = out_0.rearrange("(g p j) i -> g p j i", p=P, j=PACK)
    o1_v = out_1.rearrange("(q t) i -> q t i", t=PACK)

    def interleave(eng, dst, src):
        n = dst.shape[1]
        if eng == "v":
            nc.vector.tensor_copy(out=dst, in_=src.rearrange("p j n -> p n j"))
        elif eng == "s":
            nc.scalar.copy(out=dst, in_=src.rearrange("p j n -> p n j"))
        else:
            w = n // CHUNKS
            for c in range(CHUNKS):
                nc.gpsimd.tensor_scalar(
                    out=dst[:, c * w : (c + 1) * w, :],
                    in0=src[:, :, c * w : (c + 1) * w].rearrange("p j n -> p n j"),
                    scalar1=1.0,
                    scalar2=0.0,
                    op0=ALU.mult,
                    op1=ALU.add,
                )

    with ExitStack() as ctx:
        const = ctx.enter_context(tc.tile_pool(name="const", bufs=1))
        ld3 = ctx.enter_context(tc.tile_pool(name="ld3", bufs=3))
        ld4 = ctx.enter_context(tc.tile_pool(name="ld4", bufs=4))
        work = ctx.enter_context(tc.tile_pool(name="work", bufs=2))
        outp = ctx.enter_context(tc.tile_pool(name="outp", bufs=3))
        psum = ctx.enter_context(tc.psum_pool(name="psum", bufs=2))

        graw = const.tile([P, PACK], BF16, name="graw")
        nc.scalar.dma_start(out=graw, in_=gamma_raw.rearrange("(q t) -> q t", t=PACK))
        c_raw = const.tile([P, PACK, D], BF16, name="c_raw")

        d2_t = []
        go_t = []
        x_t = []

        def load_group(g):
            d2_g = ld3.tile([P, PACK, U], F32, name="d2_g")
            go_g = ld3.tile([P, PACK, U], BF16, name="go_g")
            if g == 0:
                for j in range(PACK):
                    nc.sync.dma_start(out=d2_g[:, j, :], in_=d2_v[g][:, j, :])
                    nc.sync.dma_start(out=go_g[:, j, :], in_=go_v[g][:, j, :])
            else:
                nc.sync.dma_start(out=d2_g, in_=d2_v[g])
                nc.sync.dma_start(out=go_g, in_=go_v[g])
            d2_t.append(d2_g)
            go_t.append(go_g)
            if g == 0:
                nc.sync.dma_start(out=c_raw, in_=centers.rearrange("(q t) i -> q t i", t=PACK))
            x_g = ld4.tile([P, PACK, D], BF16, name="x_g")
            nc.sync.dma_start(out=x_g, in_=x_v[g])
            x_t.append(x_g)

        warm = const.tile([P, 1], F32, name="warm")
        nc.vector.memset(warm, 0.0)
        nc.scalar.activation(out=warm, in_=warm, func=ACT.Exp)
        ident = const.tile([P, P], F32, name="ident")
        make_identity(nc, ident)

        load_group(0)
        load_group(1)

        v = const.tile([P, PACK], F32, name="v")
        nc.vector.tensor_copy(out=v, in_=graw)
        nabs = const.tile([P, PACK], F32, name="nabs")
        nc.vector.scalar_tensor_tensor(out=nabs, in0=v, scalar=-1.0, in1=v, op0=ALU.mult, op1=ALU.min)
        en = const.tile([P, PACK], F32, name="en")
        nc.scalar.activation(out=en, in_=nabs, func=ACT.Exp)
        l1p = const.tile([P, PACK], F32, name="l1p")
        nc.scalar.activation(out=l1p, in_=en, func=ACT.Ln, bias=1.0)
        gam = const.tile([P, PACK], F32, name="gam")
        nc.vector.scalar_tensor_tensor(out=gam, in0=v, scalar=0.0, in1=l1p, op0=ALU.max, op1=ALU.add)
        neg_g = const.tile([P, PACK], F32, name="neg_g")
        nc.vector.tensor_scalar_mul(out=neg_g, in0=gam, scalar1=-1.0)
        m2g = const.tile([P, PACK], F32, name="m2g")
        nc.vector.tensor_scalar_mul(out=m2g, in0=gam, scalar1=-2.0)

        su_part = const.tile([P, G * PACK], F32, name="su_part")
        sb_part = const.tile([P, G * PACK], F32, name="sb_part")

        c_in = const.tile([P, D, PACK], BF16, name="c_in", align_bytes=64)
        nc.vector.tensor_copy(out=c_in, in_=c_raw.rearrange("q t i -> q i t"))
        ccodes = const.tile([P, D], U32, name="ccodes", align_bytes=64)
        csc = const.tile([P, D], U8, name="csc", align_bytes=64)
        nc.vector.quantize_mx(out=ccodes.bitcast(E4X4), scales=csc, in_=c_in.rearrange("q i t -> q (i t)"))

        tcodes = const.tile([P, G, U], U32, name="tcodes", align_bytes=64)
        tsc = const.tile([P, G, U], U8, name="tsc", align_bytes=64)
        xcodes = const.tile([P, G, D], U32, name="xcodes", align_bytes=64)
        xsc = const.tile([P, G, D], U8, name="xsc", align_bytes=64)

        dz32_t = []
        dzk_t = []

        def stage_x(g):
            qx_in = work.tile([P, D, PACK], BF16, name="qx_in", align_bytes=64)
            interleave(X3_ENG, qx_in, x_t[g])
            nc.vector.quantize_mx(
                out=xcodes[:, g, :].bitcast(E4X4), scales=xsc[:, g, :], in_=qx_in.rearrange("p i j -> p (i j)")
            )

        def stage_a(g):
            d2_g = d2_t[g]
            em = work.tile([P, PACK, GT], F32, name="em")
            for t in range(PACK):
                ps = psum.tile([P, GT], F32, name="d2T", tag="d2T")
                for j in range(PACK):
                    if j < 3:
                        nc.tensor.matmul(
                            out=ps[:, j * P : (j + 1) * P], lhsT=d2_g[:, j, t::PACK], rhs=ident, start=True, stop=True
                        )
                    else:
                        nc.tensor.transpose(ps[:, j * P : (j + 1) * P], d2_g[:, j, t::PACK], ident)
                e = outp.tile([P, GT], F32, name="e")
                nc.scalar.activation(out=e, in_=ps, func=ACT.Exp, scale=neg_g[:, t : t + 1])
                nc.vector.scalar_tensor_tensor(
                    out=em[:, t, :], in0=ps, scalar=0.0, in1=e, op0=ALU.is_gt, op1=ALU.mult
                )
            words = go_t[g].bitcast(F32)
            dz32 = work.tile([P, PACK, GT], F32, name="dz32")
            for h in range(2):
                ps = psum.tile([P, GT], F32, name="goT", tag="goT")
                for j in range(PACK):
                    nc.tensor.transpose(ps[:, j * P : (j + 1) * P], words[:, j, h::2], ident)
                pv = ps.bitcast(BF16).rearrange("q (c s) -> q c s", s=2)
                for s in range(2):
                    t = 2 * h + s
                    nc.vector.scalar_tensor_tensor(
                        out=dz32[:, t, :],
                        in0=pv[:, :, s],
                        scalar=m2g[:, t : t + 1],
                        in1=em[:, t, :],
                        op0=ALU.mult,
                        op1=ALU.mult,
                        accum_out=su_part[:, g * PACK + t : g * PACK + t + 1],
                    )
            dz32_t.append(dz32)

        def stage_b(g):
            last = LAST_ON_V and g == G - 1
            dz32 = dz32_t[g]
            x_g = x_t[g]
            qf_in = work.tile([P, GT, PACK], BF16, name="qf_in", align_bytes=64)
            interleave("v" if last else X1_ENG, qf_in, dz32)
            fcodes = work.tile([P, GT], U32, name="fcodes", align_bytes=64)
            fsc = work.tile([P, GT], U8, name="fsc", align_bytes=64)
            nc.vector.quantize_mx(out=fcodes.bitcast(E5X4), scales=fsc, in_=qf_in.rearrange("q c t -> q (c t)"))
            dzk = work.tile([P, PACK, U], BF16, name="dzk")
            for j in range(PACK):
                ps = psum.tile([P, U], F32, name="dzB", tag="dzB")
                for t in range(PACK):
                    nc.tensor.transpose(ps[:, t * P : (t + 1) * P], dz32[:, t, j * P : (j + 1) * P], ident)
                nc.scalar.activation(
                    out=dzk[:, j, :], in_=ps, func=ACT.Copy, accum_out=sb_part[:, g * PACK + j : g * PACK + j + 1]
                )
            dzk_t.append(dzk)
            o0 = outp.tile([P, PACK, D], F32, name="o0")
            for j in range(PACK):
                ps = psum.tile([P, D], F32, name="px", tag="px")
                nc.tensor.matmul_mx(
                    out=ps,
                    lhsT=fcodes[:, j * P : (j + 1) * P].bitcast(E5X4),
                    lhsT_scale=fsc[:, j * P : (j + 1) * P],
                    rhs=ccodes.bitcast(E4X4),
                    rhs_scale=csc,
                    start=True,
                    stop=True,
                )
                nc.vector.scalar_tensor_tensor(
                    out=o0[:, j, :],
                    in0=x_g[:, j, :],
                    scalar=sb_part[:, g * PACK + j : g * PACK + j + 1],
                    in1=ps,
                    op0=ALU.mult,
                    op1=ALU.subtract,
                )
                if g == G - 1:
                    nc.sync.dma_start(out=o0_v[g][:, j, :], in_=o0[:, j, :])
            if g < G - 1:
                nc.sync.dma_start(out=o0_v[g], in_=o0)

        def stage_c(g):
            last = LAST_ON_V and g == G - 1
            qt_in = work.tile([P, U, PACK], BF16, name="qt_in", align_bytes=64)
            interleave("v" if last else X2_ENG, qt_in, dzk_t[g])
            nc.vector.quantize_mx(
                out=tcodes[:, g, :].bitcast(E5X4), scales=tsc[:, g, :], in_=qt_in.rearrange("p u j -> p (u j)")
            )

        acc = []

        def mx1(g):
            for t in range(PACK):
                nc.tensor.matmul_mx(
                    out=acc[t],
                    lhsT=tcodes[:, g, t * P : (t + 1) * P].bitcast(E5X4),
                    lhsT_scale=tsc[:, g, t * P : (t + 1) * P],
                    rhs=xcodes[:, g, :].bitcast(E4X4),
                    rhs_scale=xsc[:, g, :],
                    start=(g == 0),
                    stop=(g == G - 1),
                )

        for step in range(G + 2):
            if step + 2 < G:
                load_group(step + 2)
            if step < G:
                stage_a(step)
                stage_x(step)
            if 1 <= step <= G:
                stage_b(step - 1)
            if step >= 2:
                stage_c(step - 2)
            if step == G - 1:
                for t in range(PACK):
                    acc_t = psum.tile([P, D], F32, name="acc%d" % t, tag=("d2T" if t < 2 else "goT"))
                    acc.append(acc_t)
                for g in range(G - 2):
                    mx1(g)
            if step >= G:
                mx1(step - 2)

        su = const.tile([P, PACK], F32, name="su")
        nc.vector.tensor_reduce(
            out=su, in_=su_part.rearrange("q (g t) -> q t g", t=PACK), axis=mybir.AxisListType.X, op=ALU.add
        )
        o1 = const.tile([P, PACK, D], F32, name="o1")
        for t in range(PACK):
            nc.vector.scalar_tensor_tensor(
                out=o1[:, t, :],
                in0=c_raw[:, t, :],
                scalar=su[:, t : t + 1],
                in1=acc[t],
                op0=ALU.mult,
                op1=ALU.subtract,
            )
            nc.sync.dma_start(out=o1_v[:, t, :], in_=o1[:, t, :])
